import numpy as np
import ml_dtypes


def mxq(x, axis, fmt="e4m3"):
    dtype, down = {"e4m3": (ml_dtypes.float8_e4m3fn, 7), "e5m2": (ml_dtypes.float8_e5m2, 14)}[fmt]
    v = np.moveaxis(np.asarray(x, np.float32).astype(ml_dtypes.bfloat16).astype(np.float64), axis, -1)
    blocks = v.reshape(v.shape[:-1] + (-1, 32))
    amax = np.abs(blocks).max(-1, keepdims=True)
    byte = np.maximum(np.where(amax > 0, np.frexp(amax)[1] - 1 + 127, 0) - down, 1)
    scale = np.exp2(byte - 127.0)
    codes = (blocks / scale).astype(np.float32).astype(dtype).astype(np.float64)
    return np.moveaxis((codes * scale).reshape(v.shape), -1, axis)


WIDE = False


def mx_kscale(k):
    if not WIDE:
        return np.ones(k)
    levels = np.array([10, -10, 5, -5, 0])
    if k % 512:
        return np.exp2(np.random.permutation(np.resize(levels, k // 32))).repeat(32)
    a = np.empty((k // 512, 16))
    for p in range(k // 512):
        a[p, :8] = np.random.permutation(np.resize(levels, 8))
        for g in range(8):
            far = levels[np.abs(levels - a[p, g]) >= 10]
            a[p, g + 8] = far[np.random.randint(len(far))]
    return np.exp2(a.ravel()).repeat(32)


BF16 = ml_dtypes.bfloat16


def bf(x):
    return np.asarray(x, np.float32).astype(BF16)


def f64(x):
    return np.asarray(x).astype(np.float64)


B, N, D, C, H, NS = 2, 1024, 1024, 1024, 16, 10
HD = C // H
D4 = (0.4829629131445341, 0.8365163037378079, 0.2241438680420134, -0.1294095225512604)


def causal_multiscale(x_c, scale_gain):
    g = np.exp(scale_gain - scale_gain.max(0, keepdims=True))
    gains = g / g.sum(0, keepdims=True)
    gains_exp = np.repeat(gains, HD, axis=1)
    out = np.zeros_like(x_c)
    for j in range(NS):
        d = 2 ** j
        xp = np.pad(x_c, ((0, 0), (0, 0), (3 * d, 0)))
        y = (D4[0] * xp[:, :, 0 * d:0 * d + N]
             + D4[1] * xp[:, :, 1 * d:1 * d + N]
             + D4[2] * xp[:, :, 2 * d:2 * d + N]
             + D4[3] * xp[:, :, 3 * d:3 * d + N])
        out = out + gains_exp[j][None, :, None] * y
    return out


def setup_inputs():
    s = mx_kscale(D)
    return {"x": bf(np.random.standard_normal((B, N, D)) * s),
            "k_w": bf(np.random.standard_normal((C, D)) / np.sqrt(D) / s[None, :]),
            "k_b": bf(np.random.standard_normal(C) * 0.2),
            "v_w": bf(np.random.standard_normal((C, D)) / np.sqrt(D) / s[None, :]),
            "v_b": bf(np.random.standard_normal(C) * 0.2),
            "scale_gain": bf(np.random.standard_normal((NS, H)) * 0.5)}


def core(x, k_w, k_b, v_w, v_b, scale_gain):
    xq = mxq(f64(x), 2, "e4m3")
    k = ((xq @ mxq(f64(k_w), 1, "e4m3").T) + f64(k_b)).reshape(B, N, H, HD)
    v = ((xq @ mxq(f64(v_w), 1, "e4m3").T) + f64(v_b)).reshape(B, N, H, HD)
    k_mag = np.sqrt((k * k).sum(-1, keepdims=True))
    field = v * k_mag
    x_c = field.transpose(0, 2, 3, 1).reshape(B, C, N)
    return causal_multiscale(x_c, f64(scale_gain))


def e4m3fn_bytes(y):
    return np.clip(np.asarray(y, np.float64), -448.0, 448.0).astype(np.float32).astype(ml_dtypes.float8_e4m3fn).view(np.uint8)


def reference(x, k_w, k_b, v_w, v_b, scale_gain):
    out = core(x, k_w, k_b, v_w, v_b, scale_gain)
    s = np.max(np.abs(out), axis=-1, keepdims=True) / 448.0
    return out, e4m3fn_bytes(out / s)

@@ -1,0 +1,360 @@
+from contextlib import ExitStack
+
+import concourse.mybir as mybir
+from concourse.masks import make_identity
+
+B, N, D, C, H, NS = 2, 1024, 1024, 1024, 16, 10
+HD = C // H
+T0, T1, T2, T3 = 0.4829629131445341, 0.8365163037378079, 0.2241438680420134, -0.1294095225512604
+
+FLOPS = 2 * (B * N) * D * (2 * C) + 2 * B * C * N * 4 * NS
+
+F32 = mybir.dt.float32
+BF16 = mybir.dt.bfloat16
+U32 = mybir.dt.uint32
+U8 = mybir.dt.uint8
+FP8X4 = mybir.dt.float8_e4m3fn_x4
+FP8 = mybir.dt.float8_e4m3fn
+ALU = mybir.AluOpType
+ACT = mybir.ActivationFunctionType
+AX = mybir.AxisListType
+
+P = 128
+NPASS = D // 512
+NCT = C // P
+NTG = B * 2
+
+
+def tile_causalwaveletfieldattentionbyte_pa_kernel(tc, x, k_w, k_b, v_w, v_b, scale_gain, out_0, out_1):
+    nc = tc.nc
+    with ExitStack() as ctx:
+        const = ctx.enter_context(tc.tile_pool(name="const", bufs=1))
+        keep = ctx.enter_context(tc.tile_pool(name="keep", bufs=1))
+        work = ctx.enter_context(tc.tile_pool(name="work", bufs=3))
+        psum = ctx.enter_context(tc.psum_pool(name="psum", bufs=1))
+
+        ident = const.tile([P, P], F32, name="ident", tag="ident")
+        make_identity(nc, ident[:])
+        e2 = const.tile([P, 2], F32, name="e2", tag="e2")
+        nc.vector.memset(e2[:], 0.0)
+        nc.vector.memset(e2[0:64, 0:1], 1.0)
+        nc.vector.memset(e2[64:128, 1:2], 1.0)
+        zero = const.tile([P, 1], F32, name="zero", tag="zero")
+        nc.vector.memset(zero[:], 0.0)
+
+        ipad = const.tile([P, 512], F32, name="ipad", tag="ipad")
+        nc.gpsimd.memset(ipad[:], 0.0)
+        nc.gpsimd.affine_select(out=ipad[:], in_=ipad[:], compare_op=ALU.not_equal, fill=1.0, base=256, pattern=[[-1, 512]], channel_multiplier=1)
+
+        kbrow = const.tile([P, P], BF16, name="kbrow", tag="kbrow")
+        nc.vector.memset(kbrow[:], 0.0)
+        nc.sync.dma_start(out=kbrow[0:NCT, :], in_=k_b.rearrange("(ct j) -> ct j", j=P))
+        sg_bf = const.tile([P, NS * H], BF16, name="sg_bf", tag="sg_bf")
+        nc.sync.dma_start(out=sg_bf[:], in_=scale_gain.rearrange("j h -> (j h)").partition_broadcast(P))
+        vb_bc = const.tile([P, C], BF16, name="vb_bc", tag="vb_bc")
+        kbrow32 = const.tile([P, P], F32, name="kbrow32", tag="kbrow32")
+        nc.vector.tensor_copy(out=kbrow32[:], in_=kbrow[:])
+
+        sg = const.tile([P, NS, H], F32, name="sg", tag="sg")
+        mx = const.tile([P, H], F32, name="mx", tag="mx")
+        ex = const.tile([P, NS, H], F32, name="ex", tag="ex")
+        sm = const.tile([P, H], F32, name="sm", tag="sm")
+        rsm = const.tile([P, H], F32, name="rsm", tag="rsm")
+        gall = const.tile([P, NS, H], F32, name="gall", tag="gall")
+        gs = const.tile([P, NS, NCT], F32, name="gs", tag="gs")
+        cp = const.tile([P, NS, NCT], F32, name="cp", tag="cp")
+        cq = const.tile([P, NS, NCT], F32, name="cq", tag="cq")
+
+        def gains():
+            nc.vector.tensor_copy(out=sg[:].rearrange("p j h -> p (j h)"), in_=sg_bf[:])
+            nc.vector.tensor_reduce(out=mx[:], in_=sg[:].rearrange("p j h -> p h j"), axis=AX.X, op=ALU.max)
+            nc.vector.tensor_tensor(out=sg[:], in0=sg[:], in1=mx[:].unsqueeze(1).to_broadcast([P, NS, H]), op=ALU.subtract)
+            nc.scalar.activation(out=ex[:], in_=sg[:], func=ACT.Exp)
+            nc.vector.tensor_reduce(out=sm[:], in_=ex[:].rearrange("p j h -> p h j"), axis=AX.X, op=ALU.add)
+            nc.vector.reciprocal(out=rsm[:], in_=sm[:])
+            nc.vector.tensor_tensor(out=gall[:], in0=ex[:], in1=rsm[:].unsqueeze(1).to_broadcast([P, NS, H]), op=ALU.mult)
+            gv = gall[:].rearrange("p j (ct two) -> p j ct two", two=2)
+            nc.vector.tensor_scalar(out=gs[:], in0=gv[:, :, :, 0], scalar1=e2[:, 0:1], scalar2=None, op0=ALU.mult)
+            nc.vector.scalar_tensor_tensor(out=gs[:], in0=gv[:, :, :, 1], scalar=e2[:, 1:2], in1=gs[:], op0=ALU.mult, op1=ALU.add)
+            nc.vector.tensor_scalar(out=cp[:], in0=gs[:], scalar1=T2, scalar2=None, op0=ALU.mult)
+            nc.vector.scalar_tensor_tensor(out=cp[:, 1:NS, :], in0=gs[:, 0:NS - 1, :], scalar=T1, in1=cp[:, 1:NS, :], op0=ALU.mult, op1=ALU.add)
+            nc.vector.tensor_scalar(out=cq[:], in0=gs[:], scalar1=T0, scalar2=None, op0=ALU.mult)
+
+        x_codes = keep.tile([P, NPASS, B * N], U32, name="x_codes", tag="x_codes", align_bytes=64)
+        x_sc = keep.tile([P, NPASS, B * N], U8, name="x_sc", tag="x_sc", align_bytes=64)
+        kw_codes = keep.tile([P, NPASS, C], U32, name="kw_codes", tag="kw_codes", align_bytes=64)
+        kw_sc = keep.tile([P, NPASS, C], U8, name="kw_sc", tag="kw_sc", align_bytes=64)
+        vw_codes = keep.tile([P, NPASS, C], U32, name="vw_codes", tag="vw_codes", align_bytes=64)
+        vw_sc = keep.tile([P, NPASS, C], U8, name="vw_sc", tag="vw_sc", align_bytes=64)
+        m_sb = keep.tile([P, NTG, 4, H], F32, name="m_sb", tag="m_sb")
+        f_sb = keep.tile([P, NTG * 4, C], F32, name="f_sb", tag="f_sb")
+        kb = keep.tile([P, NCT], F32, name="kb", tag="kb")
+        base = keep.tile([P, 256], F32, name="base", tag="base")
+        gmat = {}
+        for j in range(1, NS):
+            gj = keep.tile([P, 256], F32, name="g%d" % j, tag="g%d" % j)
+            gmat[j] = gj
+        tt = []
+        for h in range(H):
+            tth = keep.tile([P, 256], F32, name="tt%d" % h, tag="tt%d" % h)
+            tt.append(tth)
+
+        def mx_group(ps, l_codes, l_sc, lcol, r_codes, r_sc, rcol):
+            for g in range(NPASS):
+                nc.tensor.matmul_mx(
+                    out=ps,
+                    lhsT=l_codes[:, g, lcol:lcol + P].bitcast(FP8X4),
+                    lhsT_scale=l_sc[:, g, lcol:lcol + P],
+                    rhs=r_codes[:, g, rcol:rcol + 512].bitcast(FP8X4),
+                    rhs_scale=r_sc[:, g, rcol:rcol + 512],
+                    start=(g == 0),
+                    stop=(g == NPASS - 1),
+                )
+
+        def k_unit(tg, ct, msq):
+            kps = psum.tile([P, 512], F32, name="kps", tag="mx", bufs=2)
+            mx_group(kps[:], kw_codes, kw_sc, ct * P, x_codes, x_sc, tg * 512)
+            ksq = work.tile([P, 512], F32, name="ksq", tag="ksq")
+            nc.scalar.activation(out=ksq[:], in_=kps[:], func=ACT.Square, bias=kb[:, ct:ct + 1], scale=1.0)
+            c2 = 2 * (ct % 4)
+            for r in range(4):
+                nc.tensor.matmul(out=msq[:, r, c2:c2 + 2], lhsT=ksq[:, r * P:(r + 1) * P], rhs=e2[:], start=True, stop=True)
+
+        def v_unit(tg, r, half):
+            tau = tg * 4 + r
+            vps = psum.tile([P, 512], F32, name="vps", tag="mx", bufs=2)
+            mx_group(vps[:], x_codes, x_sc, tau * P, vw_codes, vw_sc, half * 512)
+            vbt = work.tile([P, 512], F32, name="vbt", tag="vbt")
+            nc.vector.tensor_tensor(out=vbt[:], in0=vps[:], in1=vb_bc[:, half * 512:(half + 1) * 512], op=ALU.add)
+            for h8 in range(8):
+                h = half * 8 + h8
+                nc.scalar.activation(
+                    out=f_sb[:, tau, h * HD:(h + 1) * HD],
+                    in_=vbt[:, h8 * HD:(h8 + 1) * HD],
+                    func=ACT.Copy,
+                    scale=m_sb[:, tg, r, h:h + 1],
+                )
+
+        def front_units(tg, half):
+            state = {}
+
+            def k_piece(i):
+                if i == 0:
+                    msq = psum.tile([P, 4, 8], F32, name="msq", tag="msq", bufs=1)
+                    state["msq"] = msq
+                k_unit(tg, 4 * half + i, state["msq"])
+                if i == 3:
+                    nc.scalar.activation(out=m_sb[:, tg, :, half * 8:(half + 1) * 8], in_=state["msq"][:], func=ACT.Sqrt)
+
+            pieces = []
+            for i in range(4):
+                pieces.append((k_piece, i))
+            for r in range(4):
+                pieces.append((lambda rr: v_unit(tg, rr, half), r))
+            return pieces
+
+        def run(pieces):
+            for (fn, arg) in pieces:
+                fn(arg)
+
+        with ExitStack() as front:
+            raw_pool = front.enter_context(tc.tile_pool(name="raw", bufs=6))
+            grp = front.enter_context(tc.tile_pool(name="grp", bufs=3))
+
+            def load(view, nm):
+                t = raw_pool.tile([P, 4, D], BF16, name=nm, tag="raw")
+                for a in range(2):
+                    nc.sync.dma_start(out=t[:, 2 * a:2 * a + 2, :], in_=view[:, 2 * a:2 * a + 2, :])
+                return t
+
+            def w_view(w, half):
+                return w[512 * half:512 * (half + 1), :].rearrange("(s j) d -> j s d", j=P)
+
+            def x_view(tg):
+                b, hi = divmod(tg, 2)
+                return x[b, 512 * hi:512 * (hi + 1), :].rearrange("(q r) d -> q r d", r=4)
+
+            raw_kw0 = load(w_view(k_w, 0), "raw_kw0")
+            raw_x = [load(x_view(0), "raw_x0")]
+            raw_vw0 = load(w_view(v_w, 0), "raw_vw0")
+            nc.sync.dma_start(out=vb_bc[:], in_=v_b.partition_broadcast(P))
+            for tg in range(1, NTG):
+                raw_x.append(load(x_view(tg), "raw_x%d" % tg))
+            raw_kw1 = load(w_view(k_w, 1), "raw_kw1")
+            raw_vw1 = load(w_view(v_w, 1), "raw_vw1")
+
+            kbT = psum.tile([P, P], F32, name="kbT", tag="tp", bufs=1)
+            nc.tensor.transpose(kbT[:], kbrow32[:], ident[:])
+            nc.vector.tensor_copy(out=kb[:], in_=kbT[:, 0:NCT])
+
+            def prep(raw, codes, scales, col0):
+                for g in range(NPASS):
+                    grouped = grp.tile([P, 2048], BF16, name="grouped", tag="grouped", align_bytes=64)
+                    gw = grouped[:].bitcast(F32).rearrange("p (s j u) -> p s j u", s=4, u=2)
+                    for a in range(2):
+                        xt = psum.tile([P, 2, 2, P], F32, name="xt", tag=("yt" if a == 0 else "yp"), bufs=2)
+                        for s2 in range(2):
+                            words = raw[:, 2 * a + s2, :].bitcast(F32)
+                            for u in range(2):
+                                nc.tensor.transpose(xt[:, s2, u, :], words[:, 256 * g + u:256 * (g + 1):2], ident[:])
+                        src = xt[:].rearrange("p s u j -> p s j u")
+                        nc.scalar.copy(out=gw[:, 2 * a:2 * a + 2], in_=src)
+                    nc.vector.quantize_mx(
+                        out=codes[:, g, col0:col0 + 512].bitcast(FP8X4),
+                        scales=scales[:, g, col0:col0 + 512],
+                        in_=grouped[:],
+                    )
+
+            prep(raw_kw0, kw_codes, kw_sc, 0)
+            prep(raw_x[0], x_codes, x_sc, 0)
+            gains()
+            first = front_units(0, 0)
+            run(first[0:4])
+            prep(raw_vw0, vw_codes, vw_sc, 0)
+            run(first[4:8])
+            for tg in range(1, NTG):
+                prep(raw_x[tg], x_codes, x_sc, tg * 512)
+                run(front_units(tg, 0))
+            prep(raw_kw1, kw_codes, kw_sc, 512)
+            prep(raw_vw1, vw_codes, vw_sc, 512)
+
+        def shifted(d, lo, hi):
+            return ipad[:, 256 - d + lo:256 - d + hi]
+
+        nc.vector.tensor_scalar(out=base[:], in0=shifted(0, 0, 256), scalar1=T3, scalar2=None, op0=ALU.mult)
+        grange = {}
+        nc.vector.tensor_scalar(out=gmat[1][:], in0=shifted(1, 0, 256), scalar1=T1, scalar2=None, op0=ALU.mult)
+        grange[1] = (0, 256)
+        for j in range(2, NS):
+            dq = 2 ** (j - 2)
+            lo, hi = dq, min(256, 3 * dq + P)
+            gj = gmat[j]
+            nc.vector.tensor_scalar(out=gj[:, lo:hi], in0=shifted(dq, lo, hi), scalar1=T2, scalar2=None, op0=ALU.mult)
+            if 2 * dq < 256:
+                nc.vector.scalar_tensor_tensor(out=gj[:, lo:hi], in0=shifted(2 * dq, lo, hi), scalar=T1, in1=gj[:, lo:hi], op0=ALU.mult, op1=ALU.add)
+            if 3 * dq < 256:
+                nc.vector.scalar_tensor_tensor(out=gj[:, lo:hi], in0=shifted(3 * dq, lo, hi), scalar=T0, in1=gj[:, lo:hi], op0=ALU.mult, op1=ALU.add)
+            grange[j] = (lo, hi)
+
+        def build_tt(h0):
+            for j in range(1, NS):
+                lo, hi = grange[j]
+                for h in range(h0, h0 + 4):
+                    nc.vector.scalar_tensor_tensor(
+                        out=tt[h][:, lo:hi],
+                        in0=gmat[j][:, lo:hi],
+                        scalar=gall[:, j, h:h + 1],
+                        in1=(base[:, lo:hi] if j == 1 else tt[h][:, lo:hi]),
+                        op0=ALU.mult,
+                        op1=ALU.add,
+                    )
+
+        build_tt(0)
+        build_tt(4)
+
+        PAD = 8
+        vtaps = ((2, cp, 1), (3, cq, 0), (6, cq, 1))
+
+        with ExitStack() as rear:
+            back = rear.enter_context(tc.tile_pool(name="back", bufs=3))
+            small = rear.enter_context(tc.tile_pool(name="small", bufs=4))
+            ft_bufs = []
+            for i in range(4):
+                ftb = back.tile([P, PAD + N], F32, name="ft%d" % i, tag="ft%d" % i, bufs=1)
+                nc.gpsimd.memset(ftb[:, 0:PAD], 0.0)
+                ft_bufs.append(ftb)
+            f5 = f_sb[:].rearrange("p (b a r) c -> p b a r c", b=B, a=2)
+
+            def toeplitz(ct, h2, hi, yts):
+                h = 2 * ct + h2
+                cols = slice(h * HD, (h + 1) * HD)
+                yt = psum.tile([P, B, 4, HD], F32, name="yt", tag="yt", bufs=2)
+                if hi == 0:
+                    nc.tensor.matmul(out=yt[:], lhsT=tt[h][:, 0:P], rhs=f5[:, :, 0, :, cols], start=True, stop=True)
+                else:
+                    nc.tensor.matmul(out=yt[:], lhsT=tt[h][:, 0:P], rhs=f5[:, :, 1, :, cols], start=True, stop=False)
+                    nc.tensor.matmul(out=yt[:], lhsT=tt[h][:, P:2 * P], rhs=f5[:, :, 0, :, cols], start=False, stop=True)
+                nc.scalar.copy(out=yts[:, :, hi * 4:(hi + 1) * 4, h2 * HD:(h2 + 1) * HD], in_=yt[:])
+
+            def turn_f(ct, b, hi, ft, tag):
+                tp = psum.tile([P, 4, P], F32, name="tp", tag=tag, bufs=(1 if tag == "tp" else 2))
+                for r in range(4):
+                    tau = (b * 2 + hi) * 4 + r
+                    nc.tensor.transpose(tp[:, r, :], f_sb[:, tau, ct * P:(ct + 1) * P], ident[:])
+                nc.scalar.copy(
+                    out=ft[:, PAD + hi * 512:PAD + (hi + 1) * 512].rearrange("p (q r) -> p q r", r=4),
+                    in_=tp[:].rearrange("p r q -> p q r"),
+                )
+
+            def turn_y(ct, b, hi, yts, ft, acc):
+                yp = psum.tile([P, 4, P], F32, name="yp", tag="yp", bufs=2)
+                for r in range(4):
+                    nc.tensor.transpose(yp[:, r, :], yts[:, b, hi * 4 + r, :], ident[:])
+                nc.vector.scalar_tensor_tensor(
+                    out=acc[:, hi * 512:(hi + 1) * 512].rearrange("p (q r) -> p q r", r=4),
+                    in0=ft[:, PAD - 1 + hi * 512:PAD - 1 + (hi + 1) * 512].rearrange("p (q r) -> p q r", r=4),
+                    scalar=cp[:, 0, ct:ct + 1],
+                    in1=yp[:].rearrange("p r q -> p q r"),
+                    op0=ALU.mult,
+                    op1=ALU.add,
+                )
+
+            def finish(ct, fts, accs):
+                for (o, coef, j) in vtaps:
+                    for b in range(B):
+                        nc.vector.scalar_tensor_tensor(
+                            out=accs[b][:],
+                            in0=fts[b][:, PAD - o:PAD - o + N],
+                            scalar=coef[:, j, ct:ct + 1],
+                            in1=accs[b][:],
+                            op0=ALU.mult,
+                            op1=ALU.add,
+                        )
+                am = small.tile([P, B], F32, name="am", tag="am")
+                for b in range(B):
+                    nc.sync.dma_start(out=out_0[b, ct * P:(ct + 1) * P, :], in_=accs[b][:])
+                    nc.vector.tensor_reduce(out=am[:, b:b + 1], in_=accs[b][:], axis=AX.X, op=ALU.max, apply_absolute_value=True)
+                rc = small.tile([P, B], F32, name="rc", tag="rc")
+                nc.vector.reciprocal(out=rc[:], in_=am[:])
+                rs = small.tile([P, B], F32, name="rs", tag="rs")
+                nc.vector.tensor_scalar(out=rs[:], in0=rc[:], scalar1=448.0, scalar2=None, op0=ALU.mult)
+                for b in range(B):
+                    o8 = back.tile([P, N], FP8, name="o8", tag="o8", bufs=4)
+                    nc.scalar.activation(out=o8[:], in_=accs[b][:], func=ACT.Identity, bias=zero[:, 0:1], scale=rs[:, b:b + 1], saturate=False)
+                    nc.sync.dma_start(out=out_1[b, ct * P:(ct + 1) * P, :], in_=o8[:].bitcast(U8))
+
+            def start_pair(ct):
+                yts = back.tile([P, B, 8, P], F32, name="yts", tag="yts")
+                return (ct, yts, (ft_bufs[(2 * ct) % 4], ft_bufs[(2 * ct + 1) % 4]))
+
+            def weave(cur, nxt, units, tp_tag):
+                accs = []
+                if cur is not None:
+                    for b in range(B):
+                        acc = back.tile([P, N], F32, name="acc", tag="acc", bufs=4)
+                        accs.append(acc)
+                for k in range(4):
+                    k1, k0 = divmod(k, 2)
+                    if cur is not None:
+                        turn_y(cur[0], k1, k0, cur[1], cur[2][k1], accs[k1])
+                    if nxt is not None:
+                        toeplitz(nxt[0], k1, k0, nxt[1])
+                        turn_f(nxt[0], k1, k0, nxt[2][k1], tp_tag)
+                    run(units[2 * k:2 * k + 2])
+                if cur is not None:
+                    finish(cur[0], cur[2], accs)
+
+            late = []
+            for tg in range(NTG):
+                late.extend(front_units(tg, 1))
+            cur = None
+            for ct in range(NCT + 1):
+                nxt = start_pair(ct) if ct < NCT else None
+                units = late[8 * (ct - 1):8 * ct] if 1 <= ct <= 4 else []
+                if ct == 4:
+                    run(units)
+                    units = []
+                weave(cur, nxt, units, "tp" if ct <= 4 else "mx")
+                if ct in (1, 2):
+                    build_tt(4 + 4 * ct)
+                cur = nxt

@@ -42,9 +42,11 @@ def tile_causalwaveletfieldattentionbyte_pa_kernel(tc, x, k_w, k_b, v_w, v_b, sc
         zero = const.tile([P, 1], F32, name="zero", tag="zero")
         nc.vector.memset(zero[:], 0.0)
 
-        ipad = const.tile([P, 512], F32, name="ipad", tag="ipad")
-        nc.gpsimd.memset(ipad[:], 0.0)
-        nc.gpsimd.affine_select(out=ipad[:], in_=ipad[:], compare_op=ALU.not_equal, fill=1.0, base=256, pattern=[[-1, 512]], channel_multiplier=1)
+        ipq = const.tile([P, 288], F32, name="ipq", tag="ipq")
+        nc.gpsimd.memset(ipq[:], 0.0)
+        nc.vector.tensor_reduce(out=ipq[:, 128:160], in_=ident[:].rearrange("p (a s) -> p s a", a=4), axis=AX.X, op=ALU.add)
+        e4 = const.tile([P, 4], F32, name="e4", tag="e4")
+        nc.vector.tensor_reduce(out=e4[:], in_=ident[:].rearrange("p (a s) -> p a s", a=4), axis=AX.X, op=ALU.add)
 
         kbrow = const.tile([P, P], BF16, name="kbrow", tag="kbrow")
         nc.vector.memset(kbrow[:], 0.0)
@@ -64,6 +66,7 @@ def tile_causalwaveletfieldattentionbyte_pa_kernel(tc, x, k_w, k_b, v_w, v_b, sc
         gs = const.tile([P, NS, NCT], F32, name="gs", tag="gs")
         cp = const.tile([P, NS, NCT], F32, name="cp", tag="cp")
         cq = const.tile([P, NS, NCT], F32, name="cq", tag="cq")
+        gq = const.tile([P, NS, 4], F32, name="gq", tag="gq")
 
         def gains():
             nc.vector.tensor_copy(out=sg[:].rearrange("p j h -> p (j h)"), in_=sg_bf[:])
@@ -79,6 +82,10 @@ def tile_causalwaveletfieldattentionbyte_pa_kernel(tc, x, k_w, k_b, v_w, v_b, sc
             nc.vector.tensor_scalar(out=cp[:], in0=gs[:], scalar1=T2, scalar2=None, op0=ALU.mult)
             nc.vector.scalar_tensor_tensor(out=cp[:, 1:NS, :], in0=gs[:, 0:NS - 1, :], scalar=T1, in1=cp[:, 1:NS, :], op0=ALU.mult, op1=ALU.add)
             nc.vector.tensor_scalar(out=cq[:], in0=gs[:], scalar1=T0, scalar2=None, op0=ALU.mult)
+            gv4 = gall[:].rearrange("p j (q a) -> p j q a", a=4)
+            nc.vector.tensor_scalar(out=gq[:], in0=gv4[:, :, :, 0], scalar1=e4[:, 0:1], scalar2=None, op0=ALU.mult)
+            for a in range(1, 4):
+                nc.vector.scalar_tensor_tensor(out=gq[:], in0=gv4[:, :, :, a], scalar=e4[:, a:a + 1], in1=gq[:], op0=ALU.mult, op1=ALU.add)
 
         x_codes = keep.tile([P, NPASS, B * N], U32, name="x_codes", tag="x_codes", align_bytes=64)
         x_sc = keep.tile([P, NPASS, B * N], U8, name="x_sc", tag="x_sc", align_bytes=64)
@@ -89,15 +96,65 @@ def tile_causalwaveletfieldattentionbyte_pa_kernel(tc, x, k_w, k_b, v_w, v_b, sc
         m_sb = keep.tile([P, NTG, 4, H], F32, name="m_sb", tag="m_sb")
         f_sb = keep.tile([P, NTG * 4, C], F32, name="f_sb", tag="f_sb")
         kb = keep.tile([P, NCT], F32, name="kb", tag="kb")
-        base = keep.tile([P, 256], F32, name="base", tag="base")
+        taps_of = {1: ((1, T1),)}
+        for j in range(2, NS):
+            dq = 2 ** (j - 2)
+            taps_of[j] = tuple((m * dq, t) for (m, t) in ((1, T2), (2, T1), (3, T0)) if m * dq < 256)
+        grange = {}
         gmat = {}
         for j in range(1, NS):
-            gj = keep.tile([P, 256], F32, name="g%d" % j, tag="g%d" % j)
+            lo = 224 - taps_of[j][-1][0]
+            hi = 256 - taps_of[j][0][0]
+            grange[j] = (lo, hi)
+            gj = keep.tile([P, hi - lo], F32, name="g%d" % j, tag="g%d" % j)
             gmat[j] = gj
-        tt = []
-        for h in range(H):
-            tth = keep.tile([P, 256], F32, name="tt%d" % h, tag="tt%d" % h)
-            tt.append(tth)
+        strip = []
+        ttq = []
+        for hq in range(4):
+            st = keep.tile([P, 352], F32, name="strip%d" % hq, tag="strip%d" % hq)
+            nc.gpsimd.memset(st[:], 0.0)
+            strip.append(st)
+            tq = keep.tile([P, 4, 256], F32, name="ttq%d" % hq, tag="ttq%d" % hq)
+            ttq.append(tq)
+
+        def diag(d, lo, hi):
+            return ipq[:, lo + d - 96:hi + d - 96]
+
+        def build_masks():
+            for j in range(1, NS):
+                lo, hi = grange[j]
+                for i, (d, t) in enumerate(taps_of[j]):
+                    if i == 0:
+                        nc.vector.tensor_scalar(out=gmat[j][:], in0=diag(d, lo, hi), scalar1=t, scalar2=None, op0=ALU.mult)
+                    else:
+                        nc.vector.scalar_tensor_tensor(out=gmat[j][:], in0=diag(d, lo, hi), scalar=t, in1=gmat[j][:], op0=ALU.mult, op1=ALU.add)
+
+        def build_strips():
+            for hq in range(4):
+                nc.vector.tensor_scalar(out=strip[hq][:, 224:256], in0=diag(0, 224, 256), scalar1=T3, scalar2=None, op0=ALU.mult)
+            for j in range(1, NS):
+                lo, hi = grange[j]
+                for hq in range(4):
+                    nc.vector.scalar_tensor_tensor(
+                        out=strip[hq][:, lo:hi],
+                        in0=gmat[j][:],
+                        scalar=gq[:, j, hq:hq + 1],
+                        in1=strip[hq][:, lo:hi],
+                        op0=ALU.mult,
+                        op1=ALU.add,
+                    )
+
+        def turn_strips():
+            for hq in range(4):
+                for half in range(2):
+                    tps = psum.tile([P, 4, P], F32, name="tps", tag=("yt" if half == 0 else "yp"), bufs=2)
+                    for b4 in range(4):
+                        off = 224 - 32 * (4 * half + b4)
+                        nc.tensor.transpose(tps[:, b4, :], strip[hq][:, off:off + P], ident[:])
+                    nc.scalar.copy(
+                        out=ttq[hq][:, :, half * P:(half + 1) * P].rearrange("p a (b s) -> p a b s", s=32),
+                        in_=tps[:].rearrange("p b (a s) -> p a b s", s=32),
+                    )
 
         def mx_group(ps, l_codes, l_sc, lcol, r_codes, r_sc, rcol):
             for g in range(NPASS):
@@ -205,9 +262,11 @@ def tile_causalwaveletfieldattentionbyte_pa_kernel(tc, x, k_w, k_b, v_w, v_b, sc
                         in_=grouped[:],
                     )
 
+            build_masks()
             prep(raw_kw0, kw_codes, kw_sc, 0)
             prep(raw_x[0], x_codes, x_sc, 0)
             gains()
+            build_strips()
             first = front_units(0, 0)
             run(first[0:4])
             prep(raw_vw0, vw_codes, vw_sc, 0)
@@ -215,42 +274,10 @@ def tile_causalwaveletfieldattentionbyte_pa_kernel(tc, x, k_w, k_b, v_w, v_b, sc
             for tg in range(1, NTG):
                 prep(raw_x[tg], x_codes, x_sc, tg * 512)
                 run(front_units(tg, 0))
+                if tg == 1:
+                    turn_strips()
             prep(raw_kw1, kw_codes, kw_sc, 512)
             prep(raw_vw1, vw_codes, vw_sc, 512)
-
-        def shifted(d, lo, hi):
-            return ipad[:, 256 - d + lo:256 - d + hi]
-
-        nc.vector.tensor_scalar(out=base[:], in0=shifted(0, 0, 256), scalar1=T3, scalar2=None, op0=ALU.mult)
-        grange = {}
-        nc.vector.tensor_scalar(out=gmat[1][:], in0=shifted(1, 0, 256), scalar1=T1, scalar2=None, op0=ALU.mult)
-        grange[1] = (0, 256)
-        for j in range(2, NS):
-            dq = 2 ** (j - 2)
-            lo, hi = dq, min(256, 3 * dq + P)
-            gj = gmat[j]
-            nc.vector.tensor_scalar(out=gj[:, lo:hi], in0=shifted(dq, lo, hi), scalar1=T2, scalar2=None, op0=ALU.mult)
-            if 2 * dq < 256:
-                nc.vector.scalar_tensor_tensor(out=gj[:, lo:hi], in0=shifted(2 * dq, lo, hi), scalar=T1, in1=gj[:, lo:hi], op0=ALU.mult, op1=ALU.add)
-            if 3 * dq < 256:
-                nc.vector.scalar_tensor_tensor(out=gj[:, lo:hi], in0=shifted(3 * dq, lo, hi), scalar=T0, in1=gj[:, lo:hi], op0=ALU.mult, op1=ALU.add)
-            grange[j] = (lo, hi)
-
-        def build_tt(h0):
-            for j in range(1, NS):
-                lo, hi = grange[j]
-                for h in range(h0, h0 + 4):
-                    nc.vector.scalar_tensor_tensor(
-                        out=tt[h][:, lo:hi],
-                        in0=gmat[j][:, lo:hi],
-                        scalar=gall[:, j, h:h + 1],
-                        in1=(base[:, lo:hi] if j == 1 else tt[h][:, lo:hi]),
-                        op0=ALU.mult,
-                        op1=ALU.add,
-                    )
-
-        build_tt(0)
-        build_tt(4)
 
         PAD = 8
         vtaps = ((2, cp, 1), (3, cq, 0), (6, cq, 1))
@@ -268,12 +295,13 @@ def tile_causalwaveletfieldattentionbyte_pa_kernel(tc, x, k_w, k_b, v_w, v_b, sc
             def toeplitz(ct, h2, hi, yts):
                 h = 2 * ct + h2
                 cols = slice(h * HD, (h + 1) * HD)
+                th = ttq[h // 4][:, h % 4, :]
                 yt = psum.tile([P, B, 4, HD], F32, name="yt", tag="yt", bufs=2)
                 if hi == 0:
-                    nc.tensor.matmul(out=yt[:], lhsT=tt[h][:, 0:P], rhs=f5[:, :, 0, :, cols], start=True, stop=True)
+                    nc.tensor.matmul(out=yt[:], lhsT=th[:, 0:P], rhs=f5[:, :, 0, :, cols], start=True, stop=True)
                 else:
-                    nc.tensor.matmul(out=yt[:], lhsT=tt[h][:, 0:P], rhs=f5[:, :, 1, :, cols], start=True, stop=False)
-                    nc.tensor.matmul(out=yt[:], lhsT=tt[h][:, P:2 * P], rhs=f5[:, :, 0, :, cols], start=False, stop=True)
+                    nc.tensor.matmul(out=yt[:], lhsT=th[:, 0:P], rhs=f5[:, :, 1, :, cols], start=True, stop=False)
+                    nc.tensor.matmul(out=yt[:], lhsT=th[:, P:2 * P], rhs=f5[:, :, 0, :, cols], start=False, stop=True)
                 nc.scalar.copy(out=yts[:, :, hi * 4:(hi + 1) * 4, h2 * HD:(h2 + 1) * HD], in_=yt[:])
 
             def turn_f(ct, b, hi, ft, tag):
@@ -355,6 +383,4 @@ def tile_causalwaveletfieldattentionbyte_pa_kernel(tc, x, k_w, k_b, v_w, v_b, sc
                     run(units)
                     units = []
                 weave(cur, nxt, units, "tp" if ct <= 4 else "mx")
-                if ct in (1, 2):
-                    build_tt(4 + 4 * ct)
                 cur = nxt

@@ -48,14 +48,10 @@ def tile_causalwaveletfieldattentionbyte_pa_kernel(tc, x, k_w, k_b, v_w, v_b, sc
         e4 = const.tile([P, 4], F32, name="e4", tag="e4")
         nc.vector.tensor_reduce(out=e4[:], in_=ident[:].rearrange("p (a s) -> p a s", a=4), axis=AX.X, op=ALU.add)
 
-        kbrow = const.tile([P, P], BF16, name="kbrow", tag="kbrow")
-        nc.vector.memset(kbrow[:], 0.0)
-        nc.sync.dma_start(out=kbrow[0:NCT, :], in_=k_b.rearrange("(ct j) -> ct j", j=P))
         sg_bf = const.tile([P, NS * H], BF16, name="sg_bf", tag="sg_bf")
         nc.sync.dma_start(out=sg_bf[:], in_=scale_gain.rearrange("j h -> (j h)").partition_broadcast(P))
+        kb_bc = const.tile([P, C], BF16, name="kb_bc", tag="kb_bc")
         vb_bc = const.tile([P, C], BF16, name="vb_bc", tag="vb_bc")
-        kbrow32 = const.tile([P, P], F32, name="kbrow32", tag="kbrow32")
-        nc.vector.tensor_copy(out=kbrow32[:], in_=kbrow[:])
 
         sg = const.tile([P, NS, H], F32, name="sg", tag="sg")
         mx = const.tile([P, H], F32, name="mx", tag="mx")
@@ -93,9 +89,8 @@ def tile_causalwaveletfieldattentionbyte_pa_kernel(tc, x, k_w, k_b, v_w, v_b, sc
         kw_sc = keep.tile([P, NPASS, C], U8, name="kw_sc", tag="kw_sc", align_bytes=64)
         vw_codes = keep.tile([P, NPASS, C], U32, name="vw_codes", tag="vw_codes", align_bytes=64)
         vw_sc = keep.tile([P, NPASS, C], U8, name="vw_sc", tag="vw_sc", align_bytes=64)
-        m_sb = keep.tile([P, NTG, 4, H], F32, name="m_sb", tag="m_sb")
+        m_sb = keep.tile([P, NTG * 4, H], F32, name="m_sb", tag="m_sb")
         f_sb = keep.tile([P, NTG * 4, C], F32, name="f_sb", tag="f_sb")
-        kb = keep.tile([P, NCT], F32, name="kb", tag="kb")
         taps_of = {1: ((1, T1),)}
         for j in range(2, NS):
             dq = 2 ** (j - 2)
@@ -168,46 +163,35 @@ def tile_causalwaveletfieldattentionbyte_pa_kernel(tc, x, k_w, k_b, v_w, v_b, sc
                     stop=(g == NPASS - 1),
                 )
 
-        def k_unit(tg, ct, msq):
-            kps = psum.tile([P, 512], F32, name="kps", tag="mx", bufs=2)
-            mx_group(kps[:], kw_codes, kw_sc, ct * P, x_codes, x_sc, tg * 512)
-            ksq = work.tile([P, 512], F32, name="ksq", tag="ksq")
-            nc.scalar.activation(out=ksq[:], in_=kps[:], func=ACT.Square, bias=kb[:, ct:ct + 1], scale=1.0)
-            c2 = 2 * (ct % 4)
-            for r in range(4):
-                nc.tensor.matmul(out=msq[:, r, c2:c2 + 2], lhsT=ksq[:, r * P:(r + 1) * P], rhs=e2[:], start=True, stop=True)
-
-        def v_unit(tg, r, half):
-            tau = tg * 4 + r
-            vps = psum.tile([P, 512], F32, name="vps", tag="mx", bufs=2)
+        def kv_unit(tau, half):
+            cols = slice(half * 512, (half + 1) * 512)
+            kps = psum.tile([P, 512], F32, name="kps", tag="mx", bufs=3)
+            mx_group(kps[:], x_codes, x_sc, tau * P, kw_codes, kw_sc, half * 512)
+            vps = psum.tile([P, 512], F32, name="vps", tag="mx", bufs=3)
             mx_group(vps[:], x_codes, x_sc, tau * P, vw_codes, vw_sc, half * 512)
+            kbt = work.tile([P, 512], F32, name="kbt", tag="kbt")
+            nc.vector.tensor_tensor(out=kbt[:], in0=kps[:], in1=kb_bc[:, cols], op=ALU.add)
             vbt = work.tile([P, 512], F32, name="vbt", tag="vbt")
-            nc.vector.tensor_tensor(out=vbt[:], in0=vps[:], in1=vb_bc[:, half * 512:(half + 1) * 512], op=ALU.add)
+            nc.vector.tensor_tensor(out=vbt[:], in0=vps[:], in1=vb_bc[:, cols], op=ALU.add)
+            ksq = work.tile([P, 512], F32, name="ksq", tag="ksq")
+            msq = work.tile([P, 8], F32, name="msq", tag="msq")
+            for h8 in range(8):
+                hs = slice(h8 * HD, (h8 + 1) * HD)
+                nc.scalar.activation(out=ksq[:, hs], in_=kbt[:, hs], func=ACT.Square, accum_out=msq[:, h8:h8 + 1])
+            nc.scalar.activation(out=m_sb[:, tau, half * 8:(half + 1) * 8], in_=msq[:], func=ACT.Sqrt)
             for h8 in range(8):
                 h = half * 8 + h8
                 nc.scalar.activation(
                     out=f_sb[:, tau, h * HD:(h + 1) * HD],
                     in_=vbt[:, h8 * HD:(h8 + 1) * HD],
                     func=ACT.Copy,
-                    scale=m_sb[:, tg, r, h:h + 1],
+                    scale=m_sb[:, tau, h:h + 1],
                 )
 
         def front_units(tg, half):
-            state = {}
-
-            def k_piece(i):
-                if i == 0:
-                    msq = psum.tile([P, 4, 8], F32, name="msq", tag="msq", bufs=1)
-                    state["msq"] = msq
-                k_unit(tg, 4 * half + i, state["msq"])
-                if i == 3:
-                    nc.scalar.activation(out=m_sb[:, tg, :, half * 8:(half + 1) * 8], in_=state["msq"][:], func=ACT.Sqrt)
-
             pieces = []
-            for i in range(4):
-                pieces.append((k_piece, i))
             for r in range(4):
-                pieces.append((lambda rr: v_unit(tg, rr, half), r))
+                pieces.append((lambda tau: kv_unit(tau, half), tg * 4 + r))
             return pieces
 
         def run(pieces):
@@ -233,16 +217,13 @@ def tile_causalwaveletfieldattentionbyte_pa_kernel(tc, x, k_w, k_b, v_w, v_b, sc
 
             raw_kw0 = load(w_view(k_w, 0), "raw_kw0")
             raw_x = [load(x_view(0), "raw_x0")]
+            nc.sync.dma_start(out=kb_bc[:], in_=k_b.partition_broadcast(P))
             raw_vw0 = load(w_view(v_w, 0), "raw_vw0")
             nc.sync.dma_start(out=vb_bc[:], in_=v_b.partition_broadcast(P))
             for tg in range(1, NTG):
                 raw_x.append(load(x_view(tg), "raw_x%d" % tg))
             raw_kw1 = load(w_view(k_w, 1), "raw_kw1")
             raw_vw1 = load(w_view(v_w, 1), "raw_vw1")
-
-            kbT = psum.tile([P, P], F32, name="kbT", tag="tp", bufs=1)
-            nc.tensor.transpose(kbT[:], kbrow32[:], ident[:])
-            nc.vector.tensor_copy(out=kb[:], in_=kbT[:, 0:NCT])
 
             def prep(raw, codes, scales, col0):
                 for g in range(NPASS):
@@ -265,12 +246,10 @@ def tile_causalwaveletfieldattentionbyte_pa_kernel(tc, x, k_w, k_b, v_w, v_b, sc
             build_masks()
             prep(raw_kw0, kw_codes, kw_sc, 0)
             prep(raw_x[0], x_codes, x_sc, 0)
+            prep(raw_vw0, vw_codes, vw_sc, 0)
             gains()
             build_strips()
-            first = front_units(0, 0)
-            run(first[0:4])
-            prep(raw_vw0, vw_codes, vw_sc, 0)
-            run(first[4:8])
+            run(front_units(0, 0))
             for tg in range(1, NTG):
                 prep(raw_x[tg], x_codes, x_sc, tg * 512)
                 run(front_units(tg, 0))
@@ -305,7 +284,7 @@ def tile_causalwaveletfieldattentionbyte_pa_kernel(tc, x, k_w, k_b, v_w, v_b, sc
                 nc.scalar.copy(out=yts[:, :, hi * 4:(hi + 1) * 4, h2 * HD:(h2 + 1) * HD], in_=yt[:])
 
             def turn_f(ct, b, hi, ft, tag):
-                tp = psum.tile([P, 4, P], F32, name="tp", tag=tag, bufs=(1 if tag == "tp" else 2))
+                tp = psum.tile([P, 4, P], F32, name="tp", tag=tag, bufs=(1 if tag == "tp" else 3))
                 for r in range(4):
                     tau = (b * 2 + hi) * 4 + r
                     nc.tensor.transpose(tp[:, r, :], f_sb[:, tau, ct * P:(ct + 1) * P], ident[:])
@@ -368,7 +347,7 @@ def tile_causalwaveletfieldattentionbyte_pa_kernel(tc, x, k_w, k_b, v_w, v_b, sc
                     if nxt is not None:
                         toeplitz(nxt[0], k1, k0, nxt[1])
                         turn_f(nxt[0], k1, k0, nxt[2][k1], tp_tag)
-                    run(units[2 * k:2 * k + 2])
+                    run(units[k:k + 1])
                 if cur is not None:
                     finish(cur[0], cur[2], accs)
 
@@ -378,9 +357,6 @@ def tile_causalwaveletfieldattentionbyte_pa_kernel(tc, x, k_w, k_b, v_w, v_b, sc
             cur = None
             for ct in range(NCT + 1):
                 nxt = start_pair(ct) if ct < NCT else None
-                units = late[8 * (ct - 1):8 * ct] if 1 <= ct <= 4 else []
-                if ct == 4:
-                    run(units)
-                    units = []
+                units = late[4 * ct:4 * ct + 4]
                 weave(cur, nxt, units, "tp" if ct <= 4 else "mx")
                 cur = nxt

@@ -20,6 +20,12 @@ ACT = mybir.ActivationFunctionType
 AX = mybir.AxisListType
 
 P = 128
+GZ = 2
+MXB = 2
+TPB = 1
+YTB = 2
+YPB = 3
+GFIRST = 6
 NPASS = D // 512
 NCT = C // P
 NTG = B * 2
@@ -50,8 +56,7 @@ def tile_causalwaveletfieldattentionbyte_pa_kernel(tc, x, k_w, k_b, v_w, v_b, sc
 
         sg_bf = const.tile([P, NS * H], BF16, name="sg_bf", tag="sg_bf")
         nc.sync.dma_start(out=sg_bf[:], in_=scale_gain.rearrange("j h -> (j h)").partition_broadcast(P))
-        kb_bc = const.tile([P, C], BF16, name="kb_bc", tag="kb_bc")
-        vb_bc = const.tile([P, C], BF16, name="vb_bc", tag="vb_bc")
+        kvb = const.tile([P, 2, C], BF16, name="kvb", tag="kvb")
 
         sg = const.tile([P, NS, H], F32, name="sg", tag="sg")
         mx = const.tile([P, H], F32, name="mx", tag="mx")
@@ -142,7 +147,7 @@ def tile_causalwaveletfieldattentionbyte_pa_kernel(tc, x, k_w, k_b, v_w, v_b, sc
         def turn_strips():
             for hq in range(4):
                 for half in range(2):
-                    tps = psum.tile([P, 4, P], F32, name="tps", tag=("yt" if half == 0 else "yp"), bufs=2)
+                    tps = psum.tile([P, 4, P], F32, name="tps", tag=("yt" if half == 0 else "yp"), bufs=(YTB if half == 0 else YPB))
                     for b4 in range(4):
                         off = 224 - 32 * (4 * half + b4)
                         nc.tensor.transpose(tps[:, b4, :], strip[hq][:, off:off + P], ident[:])
@@ -151,47 +156,45 @@ def tile_causalwaveletfieldattentionbyte_pa_kernel(tc, x, k_w, k_b, v_w, v_b, sc
                         in_=tps[:].rearrange("p b (a s) -> p a b s", s=32),
                     )
 
-        def mx_group(ps, l_codes, l_sc, lcol, r_codes, r_sc, rcol):
+        QW = C // 4
+
+        def mx_group(ps, tau, r_codes, r_sc, rcol):
             for g in range(NPASS):
                 nc.tensor.matmul_mx(
                     out=ps,
-                    lhsT=l_codes[:, g, lcol:lcol + P].bitcast(FP8X4),
-                    lhsT_scale=l_sc[:, g, lcol:lcol + P],
-                    rhs=r_codes[:, g, rcol:rcol + 512].bitcast(FP8X4),
-                    rhs_scale=r_sc[:, g, rcol:rcol + 512],
+                    lhsT=x_codes[:, g, tau * P:(tau + 1) * P].bitcast(FP8X4),
+                    lhsT_scale=x_sc[:, g, tau * P:(tau + 1) * P],
+                    rhs=r_codes[:, g, rcol:rcol + QW].bitcast(FP8X4),
+                    rhs_scale=r_sc[:, g, rcol:rcol + QW],
                     start=(g == 0),
                     stop=(g == NPASS - 1),
                 )
 
-        def kv_unit(tau, half):
-            cols = slice(half * 512, (half + 1) * 512)
-            kps = psum.tile([P, 512], F32, name="kps", tag="mx", bufs=3)
-            mx_group(kps[:], x_codes, x_sc, tau * P, kw_codes, kw_sc, half * 512)
-            vps = psum.tile([P, 512], F32, name="vps", tag="mx", bufs=3)
-            mx_group(vps[:], x_codes, x_sc, tau * P, vw_codes, vw_sc, half * 512)
-            kbt = work.tile([P, 512], F32, name="kbt", tag="kbt")
-            nc.vector.tensor_tensor(out=kbt[:], in0=kps[:], in1=kb_bc[:, cols], op=ALU.add)
-            vbt = work.tile([P, 512], F32, name="vbt", tag="vbt")
-            nc.vector.tensor_tensor(out=vbt[:], in0=vps[:], in1=vb_bc[:, cols], op=ALU.add)
-            ksq = work.tile([P, 512], F32, name="ksq", tag="ksq")
-            msq = work.tile([P, 8], F32, name="msq", tag="msq")
-            for h8 in range(8):
-                hs = slice(h8 * HD, (h8 + 1) * HD)
-                nc.scalar.activation(out=ksq[:, hs], in_=kbt[:, hs], func=ACT.Square, accum_out=msq[:, h8:h8 + 1])
-            nc.scalar.activation(out=m_sb[:, tau, half * 8:(half + 1) * 8], in_=msq[:], func=ACT.Sqrt)
-            for h8 in range(8):
-                h = half * 8 + h8
+        def kv_unit(tau, qu):
+            kv = psum.tile([P, 2, QW], F32, name="kv", tag="mx", bufs=MXB)
+            mx_group(kv[:, 0, :], tau, kw_codes, kw_sc, qu * QW)
+            mx_group(kv[:, 1, :], tau, vw_codes, vw_sc, qu * QW)
+            kvt = work.tile([P, 2, QW], F32, name="kvt", tag="kvt")
+            nc.vector.tensor_tensor(out=kvt[:], in0=kv[:], in1=kvb[:, :, qu * QW:(qu + 1) * QW], op=ALU.add)
+            ksq = work.tile([P, QW], F32, name="ksq", tag="ksq")
+            msq = work.tile([P, 4], F32, name="msq", tag="msq")
+            for h4 in range(4):
+                hs = slice(h4 * HD, (h4 + 1) * HD)
+                nc.scalar.activation(out=ksq[:, hs], in_=kvt[:, 0, hs], func=ACT.Square, accum_out=msq[:, h4:h4 + 1])
+            nc.scalar.activation(out=m_sb[:, tau, qu * 4:(qu + 1) * 4], in_=msq[:], func=ACT.Sqrt)
+            for h4 in range(4):
+                h = qu * 4 + h4
                 nc.scalar.activation(
                     out=f_sb[:, tau, h * HD:(h + 1) * HD],
-                    in_=vbt[:, h8 * HD:(h8 + 1) * HD],
+                    in_=kvt[:, 1, h4 * HD:(h4 + 1) * HD],
                     func=ACT.Copy,
                     scale=m_sb[:, tau, h:h + 1],
                 )
 
-        def front_units(tg, half):
+        def front_units(tg, qu):
             pieces = []
             for r in range(4):
-                pieces.append((lambda tau: kv_unit(tau, half), tg * 4 + r))
+                pieces.append((lambda tau: kv_unit(tau, qu), tg * 4 + r))
             return pieces
 
         def run(pieces):
@@ -217,9 +220,9 @@ def tile_causalwaveletfieldattentionbyte_pa_kernel(tc, x, k_w, k_b, v_w, v_b, sc
 
             raw_kw0 = load(w_view(k_w, 0), "raw_kw0")
             raw_x = [load(x_view(0), "raw_x0")]
-            nc.sync.dma_start(out=kb_bc[:], in_=k_b.partition_broadcast(P))
+            nc.sync.dma_start(out=kvb[:, 0, :], in_=k_b.partition_broadcast(P))
             raw_vw0 = load(w_view(v_w, 0), "raw_vw0")
-            nc.sync.dma_start(out=vb_bc[:], in_=v_b.partition_broadcast(P))
+            nc.sync.dma_start(out=kvb[:, 1, :], in_=v_b.partition_broadcast(P))
             for tg in range(1, NTG):
                 raw_x.append(load(x_view(tg), "raw_x%d" % tg))
             raw_kw1 = load(w_view(k_w, 1), "raw_kw1")
@@ -230,7 +233,7 @@ def tile_causalwaveletfieldattentionbyte_pa_kernel(tc, x, k_w, k_b, v_w, v_b, sc
                     grouped = grp.tile([P, 2048], BF16, name="grouped", tag="grouped", align_bytes=64)
                     gw = grouped[:].bitcast(F32).rearrange("p (s j u) -> p s j u", s=4, u=2)
                     for a in range(2):
-                        xt = psum.tile([P, 2, 2, P], F32, name="xt", tag=("yt" if a == 0 else "yp"), bufs=2)
+                        xt = psum.tile([P, 2, 2, P], F32, name="xt", tag=("yt" if a == 0 else "yp"), bufs=(YTB if a == 0 else YPB))
                         for s2 in range(2):
                             words = raw[:, 2 * a + s2, :].bitcast(F32)
                             for u in range(2):
@@ -265,7 +268,7 @@ def tile_causalwaveletfieldattentionbyte_pa_kernel(tc, x, k_w, k_b, v_w, v_b, sc
             back = rear.enter_context(tc.tile_pool(name="back", bufs=3))
             small = rear.enter_context(tc.tile_pool(name="small", bufs=4))
             ft_bufs = []
-            for i in range(4):
+            for i in range(6):
                 ftb = back.tile([P, PAD + N], F32, name="ft%d" % i, tag="ft%d" % i, bufs=1)
                 nc.gpsimd.memset(ftb[:, 0:PAD], 0.0)
                 ft_bufs.append(ftb)
@@ -275,7 +278,7 @@ def tile_causalwaveletfieldattentionbyte_pa_kernel(tc, x, k_w, k_b, v_w, v_b, sc
                 h = 2 * ct + h2
                 cols = slice(h * HD, (h + 1) * HD)
                 th = ttq[h // 4][:, h % 4, :]
-                yt = psum.tile([P, B, 4, HD], F32, name="yt", tag="yt", bufs=2)
+                yt = psum.tile([P, B, 4, HD], F32, name="yt", tag="yt", bufs=YTB)
                 if hi == 0:
                     nc.tensor.matmul(out=yt[:], lhsT=th[:, 0:P], rhs=f5[:, :, 0, :, cols], start=True, stop=True)
                 else:
@@ -284,7 +287,7 @@ def tile_causalwaveletfieldattentionbyte_pa_kernel(tc, x, k_w, k_b, v_w, v_b, sc
                 nc.scalar.copy(out=yts[:, :, hi * 4:(hi + 1) * 4, h2 * HD:(h2 + 1) * HD], in_=yt[:])
 
             def turn_f(ct, b, hi, ft, tag):
-                tp = psum.tile([P, 4, P], F32, name="tp", tag=tag, bufs=(1 if tag == "tp" else 3))
+                tp = psum.tile([P, 4, P], F32, name="tp", tag=tag, bufs=(TPB if tag == "tp" else MXB))
                 for r in range(4):
                     tau = (b * 2 + hi) * 4 + r
                     nc.tensor.transpose(tp[:, r, :], f_sb[:, tau, ct * P:(ct + 1) * P], ident[:])
@@ -294,7 +297,7 @@ def tile_causalwaveletfieldattentionbyte_pa_kernel(tc, x, k_w, k_b, v_w, v_b, sc
                 )
 
             def turn_y(ct, b, hi, yts, ft, acc):
-                yp = psum.tile([P, 4, P], F32, name="yp", tag="yp", bufs=2)
+                yp = psum.tile([P, 4, P], F32, name="yp", tag="yp", bufs=YPB)
                 for r in range(4):
                     nc.tensor.transpose(yp[:, r, :], yts[:, b, hi * 4 + r, :], ident[:])
                 nc.vector.scalar_tensor_tensor(
@@ -306,57 +309,91 @@ def tile_causalwaveletfieldattentionbyte_pa_kernel(tc, x, k_w, k_b, v_w, v_b, sc
                     op1=ALU.add,
                 )
 
-            def finish(ct, fts, accs):
-                for (o, coef, j) in vtaps:
-                    for b in range(B):
-                        nc.vector.scalar_tensor_tensor(
-                            out=accs[b][:],
-                            in0=fts[b][:, PAD - o:PAD - o + N],
-                            scalar=coef[:, j, ct:ct + 1],
-                            in1=accs[b][:],
-                            op0=ALU.mult,
-                            op1=ALU.add,
-                        )
-                am = small.tile([P, B], F32, name="am", tag="am")
-                for b in range(B):
-                    nc.sync.dma_start(out=out_0[b, ct * P:(ct + 1) * P, :], in_=accs[b][:])
-                    nc.vector.tensor_reduce(out=am[:, b:b + 1], in_=accs[b][:], axis=AX.X, op=ALU.max, apply_absolute_value=True)
-                rc = small.tile([P, B], F32, name="rc", tag="rc")
+            def tap1(ct, ft, acc, i):
+                (o, coef, j) = vtaps[i]
+                nc.vector.scalar_tensor_tensor(out=acc[:], in0=ft[:, PAD - o:PAD - o + N], scalar=coef[:, j, ct:ct + 1], in1=acc[:], op0=ALU.mult, op1=ALU.add)
+
+            def close1(ct, b, acc, split):
+                nc.sync.dma_start(out=out_0[b, ct * P:(ct + 1) * P, :], in_=acc[:])
+                am = small.tile([P, 1], F32, name="am", tag="am")
+                nc.vector.tensor_reduce(out=am[:], in_=acc[:], axis=AX.X, op=ALU.max, apply_absolute_value=True)
+                rc = small.tile([P, 1], F32, name="rc", tag="rc")
                 nc.vector.reciprocal(out=rc[:], in_=am[:])
-                rs = small.tile([P, B], F32, name="rs", tag="rs")
+                rs = small.tile([P, 1], F32, name="rs", tag="rs")
                 nc.vector.tensor_scalar(out=rs[:], in0=rc[:], scalar1=448.0, scalar2=None, op0=ALU.mult)
-                for b in range(B):
-                    o8 = back.tile([P, N], FP8, name="o8", tag="o8", bufs=4)
-                    nc.scalar.activation(out=o8[:], in_=accs[b][:], func=ACT.Identity, bias=zero[:, 0:1], scale=rs[:, b:b + 1], saturate=False)
-                    nc.sync.dma_start(out=out_1[b, ct * P:(ct + 1) * P, :], in_=o8[:].bitcast(U8))
+                o8 = back.tile([P, N], FP8, name="o8", tag="o8", bufs=4)
+                cut = N // 2 if split else N
+                nc.scalar.activation(out=o8[:, 0:cut], in_=acc[:, 0:cut], func=ACT.Identity, bias=zero[:, 0:1], scale=rs[:, 0:1], saturate=False)
+                if split:
+                    nc.vector.tensor_scalar(out=o8[:, cut:N], in0=acc[:, cut:N], scalar1=rs[:, 0:1], scalar2=None, op0=ALU.mult, saturate=False)
+                nc.sync.dma_start(out=out_1[b, ct * P:(ct + 1) * P, :], in_=o8[:].bitcast(U8))
+
+            def fin_tile(t, b, part):
+                ct = t[0]
+                g = GZ if ct >= GFIRST else 0
+                steps = []
+                for i in range(3 - g):
+                    steps.append(("tap", i))
+                if g > 0:
+                    steps.append(("z", 0))
+                steps.append(("close", 0))
+                half = (len(steps) + 1) // 2
+                for (what, i) in (steps[:half] if part == 0 else steps[half:]):
+                    if what == "tap":
+                        tap1(ct, t[2][b], t[3][b], i)
+                    elif what == "z":
+                        nc.vector.tensor_tensor(out=t[3][b][:], in0=t[3][b][:], in1=t[4][b][:], op=ALU.add)
+                    else:
+                        close1(ct, b, t[3][b], ct == NCT - 1 and b == 1)
 
             def start_pair(ct):
-                yts = back.tile([P, B, 8, P], F32, name="yts", tag="yts")
-                return (ct, yts, (ft_bufs[(2 * ct) % 4], ft_bufs[(2 * ct + 1) % 4]))
-
-            def weave(cur, nxt, units, tp_tag):
+                yts = back.tile([P, B, 8, P], F32, name="yts", tag="yts", bufs=2)
                 accs = []
-                if cur is not None:
-                    for b in range(B):
-                        acc = back.tile([P, N], F32, name="acc", tag="acc", bufs=4)
-                        accs.append(acc)
+                for b in range(B):
+                    acc = back.tile([P, N], F32, name="acc", tag="acc", bufs=5)
+                    accs.append(acc)
+                return (ct, yts, (ft_bufs[(2 * ct) % 6], ft_bufs[(2 * ct + 1) % 6]), accs, [])
+
+            def gz_sum(ct, fts):
+                zs = []
+                for b in range(B):
+                    z = back.tile([P, N], F32, name="z", tag="z", bufs=3)
+                    for i in range(3 - GZ, 3):
+                        (o, coef, j) = vtaps[i]
+                        dst = z
+                        if i > 3 - GZ:
+                            dst = back.tile([P, N], F32, name="zt", tag="zt", bufs=1)
+                        nc.gpsimd.tensor_scalar(out=dst[:], in0=fts[b][:, PAD - o:PAD - o + N], scalar1=coef[:, j, ct:ct + 1], scalar2=0.0, op0=ALU.mult, op1=ALU.add)
+                        if i > 3 - GZ:
+                            nc.gpsimd.tensor_tensor(out=z[:], in0=z[:], in1=dst[:], op=ALU.add)
+                    zs.append(z)
+                return zs
+
+            def weave(fin, cur, nxt, units, tp_tag):
                 for k in range(4):
                     k1, k0 = divmod(k, 2)
                     if cur is not None:
-                        turn_y(cur[0], k1, k0, cur[1], cur[2][k1], accs[k1])
+                        turn_y(cur[0], k1, k0, cur[1], cur[2][k1], cur[3][k1])
                     if nxt is not None:
                         toeplitz(nxt[0], k1, k0, nxt[1])
                         turn_f(nxt[0], k1, k0, nxt[2][k1], tp_tag)
-                    run(units[k:k + 1])
-                if cur is not None:
-                    finish(cur[0], cur[2], accs)
+                    run(units[2 * k:2 * k + 2])
+                    if k < 2 and fin is not None:
+                        fin_tile(fin, 1, k)
+                    if k >= 2 and cur is not None:
+                        fin_tile(cur, 0, k - 2)
+                if nxt is not None and GZ > 0 and nxt[0] >= GFIRST:
+                    nxt[4].extend(gz_sum(nxt[0], nxt[2]))
 
             late = []
-            for tg in range(NTG):
-                late.extend(front_units(tg, 1))
+            for qu in range(1, 4):
+                for tg in range(NTG):
+                    late.extend(front_units(tg, qu))
+            fin = None
             cur = None
-            for ct in range(NCT + 1):
+            for ct in range(NCT + 2):
                 nxt = start_pair(ct) if ct < NCT else None
-                units = late[4 * ct:4 * ct + 4]
-                weave(cur, nxt, units, "tp" if ct <= 4 else "mx")
+                units = late[8 * ct:8 * ct + 8]
+                weave(fin, cur, nxt, units, "tp" if ct <= 5 else "mx")
+                fin = cur
                 cur = nxt

@@ -20,7 +20,7 @@ ACT = mybir.ActivationFunctionType
 AX = mybir.AxisListType
 
 P = 128
-GZ = 2
+GZ = 0
 MXB = 2
 TPB = 1
 YTB = 2
@@ -103,8 +103,8 @@ def tile_causalwaveletfieldattentionbyte_pa_kernel(tc, x, k_w, k_b, v_w, v_b, sc
         grange = {}
         gmat = {}
         for j in range(1, NS):
-            lo = 224 - taps_of[j][-1][0]
-            hi = 256 - taps_of[j][0][0]
+            lo = 96 + taps_of[j][0][0]
+            hi = 128 + taps_of[j][-1][0]
             grange[j] = (lo, hi)
             gj = keep.tile([P, hi - lo], F32, name="g%d" % j, tag="g%d" % j)
             gmat[j] = gj
@@ -118,7 +118,7 @@ def tile_causalwaveletfieldattentionbyte_pa_kernel(tc, x, k_w, k_b, v_w, v_b, sc
             ttq.append(tq)
 
         def diag(d, lo, hi):
-            return ipq[:, lo + d - 96:hi + d - 96]
+            return ipq[:, lo - d + 32:hi - d + 32]
 
         def build_masks():
             for j in range(1, NS):
@@ -131,7 +131,7 @@ def tile_causalwaveletfieldattentionbyte_pa_kernel(tc, x, k_w, k_b, v_w, v_b, sc
 
         def build_strips():
             for hq in range(4):
-                nc.vector.tensor_scalar(out=strip[hq][:, 224:256], in0=diag(0, 224, 256), scalar1=T3, scalar2=None, op0=ALU.mult)
+                nc.vector.tensor_scalar(out=strip[hq][:, 96:128], in0=diag(0, 96, 128), scalar1=T3, scalar2=None, op0=ALU.mult)
             for j in range(1, NS):
                 lo, hi = grange[j]
                 for hq in range(4):
@@ -144,17 +144,11 @@ def tile_causalwaveletfieldattentionbyte_pa_kernel(tc, x, k_w, k_b, v_w, v_b, sc
                         op1=ALU.add,
                     )
 
-        def turn_strips():
+        def spread_strips():
             for hq in range(4):
-                for half in range(2):
-                    tps = psum.tile([P, 4, P], F32, name="tps", tag=("yt" if half == 0 else "yp"), bufs=(YTB if half == 0 else YPB))
-                    for b4 in range(4):
-                        off = 224 - 32 * (4 * half + b4)
-                        nc.tensor.transpose(tps[:, b4, :], strip[hq][:, off:off + P], ident[:])
-                    nc.scalar.copy(
-                        out=ttq[hq][:, :, half * P:(half + 1) * P].rearrange("p a (b s) -> p a b s", s=32),
-                        in_=tps[:].rearrange("p b (a s) -> p a b s", s=32),
-                    )
+                for a in range(4):
+                    for b in range(4):
+                        nc.sync.dma_start(out=ttq[hq][32 * b:32 * b + 32, a, :], in_=strip[hq][32 * a:32 * a + 32, 96 - 32 * b:352 - 32 * b])
 
         QW = C // 4
 
@@ -252,12 +246,11 @@ def tile_causalwaveletfieldattentionbyte_pa_kernel(tc, x, k_w, k_b, v_w, v_b, sc
             prep(raw_vw0, vw_codes, vw_sc, 0)
             gains()
             build_strips()
+            spread_strips()
             run(front_units(0, 0))
             for tg in range(1, NTG):
                 prep(raw_x[tg], x_codes, x_sc, tg * 512)
                 run(front_units(tg, 0))
-                if tg == 1:
-                    turn_strips()
             prep(raw_kw1, kw_codes, kw_sc, 512)
             prep(raw_vw1, vw_codes, vw_sc, 512)
 
@@ -375,8 +368,8 @@ def tile_causalwaveletfieldattentionbyte_pa_kernel(tc, x, k_w, k_b, v_w, v_b, sc
                     if cur is not None:
                         turn_y(cur[0], k1, k0, cur[1], cur[2][k1], cur[3][k1])
                     if nxt is not None:
-                        toeplitz(nxt[0], k1, k0, nxt[1])
                         turn_f(nxt[0], k1, k0, nxt[2][k1], tp_tag)
+                        toeplitz(nxt[0], k1, k0, nxt[1])
                     run(units[2 * k:2 * k + 2])
                     if k < 2 and fin is not None:
                         fin_tile(fin, 1, k)

@@ -247,11 +247,14 @@ def tile_causalwaveletfieldattentionbyte_pa_kernel(tc, x, k_w, k_b, v_w, v_b, sc
             gains()
             build_strips()
             spread_strips()
+            prep(raw_x[1], x_codes, x_sc, 512)
             run(front_units(0, 0))
-            for tg in range(1, NTG):
-                prep(raw_x[tg], x_codes, x_sc, tg * 512)
-                run(front_units(tg, 0))
+            prep(raw_x[2], x_codes, x_sc, 1024)
+            run(front_units(1, 0))
+            prep(raw_x[3], x_codes, x_sc, 1536)
+            run(front_units(2, 0))
             prep(raw_kw1, kw_codes, kw_sc, 512)
+            run(front_units(3, 0))
             prep(raw_vw1, vw_codes, vw_sc, 512)
 
         PAD = 8
@@ -362,31 +365,30 @@ def tile_causalwaveletfieldattentionbyte_pa_kernel(tc, x, k_w, k_b, v_w, v_b, sc
                     zs.append(z)
                 return zs
 
-            def weave(fin, cur, nxt, units, tp_tag):
+            def weave(cur, nxt, units, tp_tag):
                 for k in range(4):
                     k1, k0 = divmod(k, 2)
-                    if cur is not None:
-                        turn_y(cur[0], k1, k0, cur[1], cur[2][k1], cur[3][k1])
+                    if k < 2 and cur is not None:
+                        turn_y(cur[0], k0, 1, cur[1], cur[2][k0], cur[3][k0])
+                    if k >= 2 and nxt is not None:
+                        turn_y(nxt[0], k0, 0, nxt[1], nxt[2][k0], nxt[3][k0])
                     if nxt is not None:
-                        turn_f(nxt[0], k1, k0, nxt[2][k1], tp_tag)
-                        toeplitz(nxt[0], k1, k0, nxt[1])
+                        turn_f(nxt[0], k0, k1, nxt[2][k0], tp_tag)
+                        toeplitz(nxt[0], k0, k1, nxt[1])
                     run(units[2 * k:2 * k + 2])
-                    if k < 2 and fin is not None:
-                        fin_tile(fin, 1, k)
-                    if k >= 2 and cur is not None:
-                        fin_tile(cur, 0, k - 2)
-                if nxt is not None and GZ > 0 and nxt[0] >= GFIRST:
-                    nxt[4].extend(gz_sum(nxt[0], nxt[2]))
+                    if cur is not None:
+                        if k in (0, 1):
+                            fin_tile(cur, 0, k)
+                        else:
+                            fin_tile(cur, 1, k - 2)
 
             late = []
             for qu in range(1, 4):
                 for tg in range(NTG):
                     late.extend(front_units(tg, qu))
-            fin = None
             cur = None
-            for ct in range(NCT + 2):
+            for ct in range(NCT + 1):
                 nxt = start_pair(ct) if ct < NCT else None
                 units = late[8 * ct:8 * ct + 8]
-                weave(fin, cur, nxt, units, "tp" if ct <= 5 else "mx")
-                fin = cur
+                weave(cur, nxt, units, "tp" if ct <= 5 else "mx")
                 cur = nxt

@@ -25,7 +25,8 @@ MXB = 2
 TPB = 1
 YTB = 2
 YPB = 3
-GFIRST = 6
+GFIRST = 8
+HELD = 1
 NPASS = D // 512
 NCT = C // P
 NTG = B * 2
@@ -296,6 +297,10 @@ def tile_causalwaveletfieldattentionbyte_pa_kernel(tc, x, k_w, k_b, v_w, v_b, sc
                 yp = psum.tile([P, 4, P], F32, name="yp", tag="yp", bufs=YPB)
                 for r in range(4):
                     nc.tensor.transpose(yp[:, r, :], yts[:, b, hi * 4 + r, :], ident[:])
+                if ct == HELD:
+                    part = acc[:, hi * 512:(hi + 1) * 512].rearrange("p (q r) -> p q r", r=4)
+                    nc.vector.tensor_tensor(out=part, in0=part, in1=yp[:].rearrange("p r q -> p q r"), op=ALU.add)
+                    return
                 nc.vector.scalar_tensor_tensor(
                     out=acc[:, hi * 512:(hi + 1) * 512].rearrange("p (q r) -> p q r", r=4),
                     in0=ft[:, PAD - 1 + hi * 512:PAD - 1 + (hi + 1) * 512].rearrange("p (q r) -> p q r", r=4),
@@ -329,7 +334,8 @@ def tile_causalwaveletfieldattentionbyte_pa_kernel(tc, x, k_w, k_b, v_w, v_b, sc
                 g = GZ if ct >= GFIRST else 0
                 steps = []
                 for i in range(3 - g):
-                    steps.append(("tap", i))
+                    if ct != HELD:
+                        steps.append(("tap", i))
                 if g > 0:
                     steps.append(("z", 0))
                 steps.append(("close", 0))
@@ -340,15 +346,17 @@ def tile_causalwaveletfieldattentionbyte_pa_kernel(tc, x, k_w, k_b, v_w, v_b, sc
                     elif what == "z":
                         nc.vector.tensor_tensor(out=t[3][b][:], in0=t[3][b][:], in1=t[4][b][:], op=ALU.add)
                     else:
-                        close1(ct, b, t[3][b], ct == NCT - 1 and b == 1)
+                        close1(ct, b, t[3][b], ct == HELD and b == 1)
 
-            def start_pair(ct):
+            def start_pair(ct, place):
                 yts = back.tile([P, B, 8, P], F32, name="yts", tag="yts", bufs=2)
+                if ct == HELD:
+                    return (ct, yts, held_fts, held_accs, [])
                 accs = []
                 for b in range(B):
                     acc = back.tile([P, N], F32, name="acc", tag="acc", bufs=5)
                     accs.append(acc)
-                return (ct, yts, (ft_bufs[(2 * ct) % 6], ft_bufs[(2 * ct + 1) % 6]), accs, [])
+                return (ct, yts, (ft_bufs[(2 * place) % 6], ft_bufs[(2 * place + 1) % 6]), accs, [])
 
             def gz_sum(ct, fts):
                 zs = []
@@ -373,9 +381,11 @@ def tile_causalwaveletfieldattentionbyte_pa_kernel(tc, x, k_w, k_b, v_w, v_b, sc
                     if k >= 2 and nxt is not None:
                         turn_y(nxt[0], k0, 0, nxt[1], nxt[2][k0], nxt[3][k0])
                     if nxt is not None:
-                        turn_f(nxt[0], k0, k1, nxt[2][k0], tp_tag)
+                        if nxt[0] != HELD:
+                            turn_f(nxt[0], k0, k1, nxt[2][k0], tp_tag)
                         toeplitz(nxt[0], k0, k1, nxt[1])
-                    run(units[2 * k:2 * k + 2])
+                    per = len(units) // 4
+                    run(units[per * k:per * (k + 1)])
                     if cur is not None:
                         if k in (0, 1):
                             fin_tile(cur, 0, k)
@@ -386,9 +396,25 @@ def tile_causalwaveletfieldattentionbyte_pa_kernel(tc, x, k_w, k_b, v_w, v_b, sc
             for qu in range(1, 4):
                 for tg in range(NTG):
                     late.extend(front_units(tg, qu))
+            held_fts = (ft_bufs[0], ft_bufs[1])
+            held_accs = []
+            for b in range(B):
+                hacc = back.tile([P, N], F32, name="hacc%d" % b, tag="hacc%d" % b, bufs=1)
+                held_accs.append(hacc)
+            for k in range(4):
+                k1, k0 = divmod(k, 2)
+                turn_f(HELD, k0, k1, held_fts[k0], "tp")
+            for b in range(B):
+                nc.vector.tensor_scalar(out=held_accs[b][:], in0=held_fts[b][:, PAD - 1:PAD - 1 + N], scalar1=cp[:, 0, HELD:HELD + 1], scalar2=None, op0=ALU.mult)
+            for i in range(3):
+                for b in range(B):
+                    tap1(HELD, held_fts[b], held_accs[b], i)
+            order = [ct for ct in range(NCT) if ct != HELD] + [HELD]
+            shares = (16, 8, 8, 8, 8)
             cur = None
-            for ct in range(NCT + 1):
-                nxt = start_pair(ct) if ct < NCT else None
-                units = late[8 * ct:8 * ct + 8]
-                weave(cur, nxt, units, "tp" if ct <= 5 else "mx")
+            for pos in range(NCT + 1):
+                nxt = start_pair(order[pos], pos + 1) if pos < NCT else None
+                first = sum(shares[:pos])
+                units = late[first:first + shares[pos]] if pos < len(shares) else []
+                weave(cur, nxt, units, "tp" if pos < len(shares) else "mx")
                 cur = nxt

@@ -223,7 +223,7 @@ def tile_causalwaveletfieldattentionbyte_pa_kernel(tc, x, k_w, k_b, v_w, v_b, sc
             raw_kw1 = load(w_view(k_w, 1), "raw_kw1")
             raw_vw1 = load(w_view(v_w, 1), "raw_vw1")
 
-            def prep(raw, codes, scales, col0):
+            def prep(raw, codes, scales, col0, shared=False):
                 for g in range(NPASS):
                     grouped = grp.tile([P, 2048], BF16, name="grouped", tag="grouped", align_bytes=64)
                     gw = grouped[:].bitcast(F32).rearrange("p (s j u) -> p s j u", s=4, u=2)
@@ -234,7 +234,10 @@ def tile_causalwaveletfieldattentionbyte_pa_kernel(tc, x, k_w, k_b, v_w, v_b, sc
                             for u in range(2):
                                 nc.tensor.transpose(xt[:, s2, u, :], words[:, 256 * g + u:256 * (g + 1):2], ident[:])
                         src = xt[:].rearrange("p s u j -> p s j u")
-                        nc.scalar.copy(out=gw[:, 2 * a:2 * a + 2], in_=src)
+                        if shared and a == 1:
+                            nc.vector.tensor_copy(out=gw[:, 2 * a:2 * a + 2], in_=src)
+                        else:
+                            nc.scalar.copy(out=gw[:, 2 * a:2 * a + 2], in_=src)
                     nc.vector.quantize_mx(
                         out=codes[:, g, col0:col0 + 512].bitcast(FP8X4),
                         scales=scales[:, g, col0:col0 + 512],
@@ -252,11 +255,11 @@ def tile_causalwaveletfieldattentionbyte_pa_kernel(tc, x, k_w, k_b, v_w, v_b, sc
             run(front_units(0, 0))
             prep(raw_x[2], x_codes, x_sc, 1024)
             run(front_units(1, 0))
-            prep(raw_x[3], x_codes, x_sc, 1536)
+            prep(raw_x[3], x_codes, x_sc, 1536, True)
             run(front_units(2, 0))
-            prep(raw_kw1, kw_codes, kw_sc, 512)
+            prep(raw_kw1, kw_codes, kw_sc, 512, True)
             run(front_units(3, 0))
-            prep(raw_vw1, vw_codes, vw_sc, 512)
+            prep(raw_vw1, vw_codes, vw_sc, 512, True)
 
         PAD = 8
         vtaps = ((2, cp, 1), (3, cq, 0), (6, cq, 1))

@@ -20,13 +20,11 @@ ACT = mybir.ActivationFunctionType
 AX = mybir.AxisListType
 
 P = 128
-GZ = 0
 MXB = 2
 TPB = 1
-YTB = 2
-YPB = 3
-GFIRST = 8
+YTB = 5
 HELD = 1
+NATB = 3
 NPASS = D // 512
 NCT = C // P
 NTG = B * 2
@@ -69,6 +67,8 @@ def tile_causalwaveletfieldattentionbyte_pa_kernel(tc, x, k_w, k_b, v_w, v_b, sc
         cp = const.tile([P, NS, NCT], F32, name="cp", tag="cp")
         cq = const.tile([P, NS, NCT], F32, name="cq", tag="cq")
         gq = const.tile([P, NS, 4], F32, name="gq", tag="gq")
+        cph = const.tile([P, NS, H], F32, name="cph", tag="cph")
+        cqh = const.tile([P, NS, H], F32, name="cqh", tag="cqh")
 
         def gains():
             nc.vector.tensor_copy(out=sg[:].rearrange("p j h -> p (j h)"), in_=sg_bf[:])
@@ -84,6 +84,9 @@ def tile_causalwaveletfieldattentionbyte_pa_kernel(tc, x, k_w, k_b, v_w, v_b, sc
             nc.vector.tensor_scalar(out=cp[:], in0=gs[:], scalar1=T2, scalar2=None, op0=ALU.mult)
             nc.vector.scalar_tensor_tensor(out=cp[:, 1:NS, :], in0=gs[:, 0:NS - 1, :], scalar=T1, in1=cp[:, 1:NS, :], op0=ALU.mult, op1=ALU.add)
             nc.vector.tensor_scalar(out=cq[:], in0=gs[:], scalar1=T0, scalar2=None, op0=ALU.mult)
+            nc.vector.tensor_scalar(out=cph[:], in0=gall[:], scalar1=T2, scalar2=None, op0=ALU.mult)
+            nc.vector.scalar_tensor_tensor(out=cph[:, 1:NS, :], in0=gall[:, 0:NS - 1, :], scalar=T1, in1=cph[:, 1:NS, :], op0=ALU.mult, op1=ALU.add)
+            nc.vector.tensor_scalar(out=cqh[:], in0=gall[:], scalar1=T0, scalar2=None, op0=ALU.mult)
             gv4 = gall[:].rearrange("p j (q a) -> p j q a", a=4)
             nc.vector.tensor_scalar(out=gq[:], in0=gv4[:, :, :, 0], scalar1=e4[:, 0:1], scalar2=None, op0=ALU.mult)
             for a in range(1, 4):
@@ -96,7 +99,8 @@ def tile_causalwaveletfieldattentionbyte_pa_kernel(tc, x, k_w, k_b, v_w, v_b, sc
         vw_codes = keep.tile([P, NPASS, C], U32, name="vw_codes", tag="vw_codes", align_bytes=64)
         vw_sc = keep.tile([P, NPASS, C], U8, name="vw_sc", tag="vw_sc", align_bytes=64)
         m_sb = keep.tile([P, NTG * 4, H], F32, name="m_sb", tag="m_sb")
-        f_sb = keep.tile([P, NTG * 4, C], F32, name="f_sb", tag="f_sb")
+        f_sb = keep.tile([P, 8, H, B, HD], F32, name="f_sb", tag="f_sb")
+        f_held = keep.tile([P, NTG * 4, P], F32, name="f_held", tag="f_held")
         taps_of = {1: ((1, T1),)}
         for j in range(2, NS):
             dq = 2 ** (j - 2)
@@ -179,8 +183,12 @@ def tile_causalwaveletfieldattentionbyte_pa_kernel(tc, x, k_w, k_b, v_w, v_b, sc
             nc.scalar.activation(out=m_sb[:, tau, qu * 4:(qu + 1) * 4], in_=msq[:], func=ACT.Sqrt)
             for h4 in range(4):
                 h = qu * 4 + h4
+                if h // 2 == HELD:
+                    dst = f_held[:, tau, (h % 2) * HD:(h % 2 + 1) * HD]
+                else:
+                    dst = f_sb[:, tau % 8, h, (tau // 8 + h) % 2, :]
                 nc.scalar.activation(
-                    out=f_sb[:, tau, h * HD:(h + 1) * HD],
+                    out=dst,
                     in_=kvt[:, 1, h4 * HD:(h4 + 1) * HD],
                     func=ACT.Copy,
                     scale=m_sb[:, tau, h:h + 1],
@@ -228,7 +236,7 @@ def tile_causalwaveletfieldattentionbyte_pa_kernel(tc, x, k_w, k_b, v_w, v_b, sc
                     grouped = grp.tile([P, 2048], BF16, name="grouped", tag="grouped", align_bytes=64)
                     gw = grouped[:].bitcast(F32).rearrange("p (s j u) -> p s j u", s=4, u=2)
                     for a in range(2):
-                        xt = psum.tile([P, 2, 2, P], F32, name="xt", tag=("yt" if a == 0 else "yp"), bufs=(YTB if a == 0 else YPB))
+                        xt = psum.tile([P, 2, 2, P], F32, name="xt", tag="yt", bufs=YTB)
                         for s2 in range(2):
                             words = raw[:, 2 * a + s2, :].bitcast(F32)
                             for u in range(2):
@@ -262,7 +270,7 @@ def tile_causalwaveletfieldattentionbyte_pa_kernel(tc, x, k_w, k_b, v_w, v_b, sc
             prep(raw_vw1, vw_codes, vw_sc, 512, True)
 
         PAD = 8
-        vtaps = ((2, cp, 1), (3, cq, 0), (6, cq, 1))
+        vtaps = ((2, 0, 1), (3, 1, 0), (6, 1, 1))
 
         with ExitStack() as rear:
             back = rear.enter_context(tc.tile_pool(name="back", bufs=3))
@@ -272,53 +280,103 @@ def tile_causalwaveletfieldattentionbyte_pa_kernel(tc, x, k_w, k_b, v_w, v_b, sc
                 ftb = back.tile([P, PAD + N], F32, name="ft%d" % i, tag="ft%d" % i, bufs=1)
                 nc.gpsimd.memset(ftb[:, 0:PAD], 0.0)
                 ft_bufs.append(ftb)
-            f5 = f_sb[:].rearrange("p (b a r) c -> p b a r c", b=B, a=2)
+            fh5 = f_held[:].rearrange("p (b a r) c -> p b a r c", b=B, a=2)
 
-            def toeplitz(ct, h2, hi, yts):
-                h = 2 * ct + h2
-                cols = slice(h * HD, (h + 1) * HD)
-                th = ttq[h // 4][:, h % 4, :]
-                yt = psum.tile([P, B, 4, HD], F32, name="yt", tag="yt", bufs=YTB)
-                if hi == 0:
-                    nc.tensor.matmul(out=yt[:], lhsT=th[:, 0:P], rhs=f5[:, :, 0, :, cols], start=True, stop=True)
-                else:
-                    nc.tensor.matmul(out=yt[:], lhsT=th[:, 0:P], rhs=f5[:, :, 1, :, cols], start=True, stop=False)
-                    nc.tensor.matmul(out=yt[:], lhsT=th[:, P:2 * P], rhs=f5[:, :, 0, :, cols], start=False, stop=True)
-                nc.scalar.copy(out=yts[:, :, hi * 4:(hi + 1) * 4, h2 * HD:(h2 + 1) * HD], in_=yt[:])
+            def f_tile(h, hi, r):
+                return f_sb[:, hi * 4 + r, h].rearrange("p s c -> p (s c)")
 
-            def turn_f(ct, b, hi, ft, tag):
+            def turn_f(h, hi, ft, tag):
                 tp = psum.tile([P, 4, P], F32, name="tp", tag=tag, bufs=(TPB if tag == "tp" else MXB))
                 for r in range(4):
-                    tau = (b * 2 + hi) * 4 + r
-                    nc.tensor.transpose(tp[:, r, :], f_sb[:, tau, ct * P:(ct + 1) * P], ident[:])
+                    nc.tensor.transpose(tp[:, r, :], f_tile(h, hi, r), ident[:])
                 nc.scalar.copy(
                     out=ft[:, PAD + hi * 512:PAD + (hi + 1) * 512].rearrange("p (q r) -> p q r", r=4),
                     in_=tp[:].rearrange("p r q -> p q r"),
                 )
 
-            def turn_y(ct, b, hi, yts, ft, acc):
-                yp = psum.tile([P, 4, P], F32, name="yp", tag="yp", bufs=YPB)
+            def toep(h, hi):
+                th = ttq[h // 4][:, h % 4, :]
+                y = psum.tile([P, 4, P], F32, name="y", tag="yt", bufs=YTB)
                 for r in range(4):
-                    nc.tensor.transpose(yp[:, r, :], yts[:, b, hi * 4 + r, :], ident[:])
-                if ct == HELD:
-                    part = acc[:, hi * 512:(hi + 1) * 512].rearrange("p (q r) -> p q r", r=4)
-                    nc.vector.tensor_tensor(out=part, in0=part, in1=yp[:].rearrange("p r q -> p q r"), op=ALU.add)
-                    return
+                    if hi == 0:
+                        nc.tensor.matmul(out=y[:, r, :], lhsT=f_tile(h, 0, r), rhs=th[:, 0:P], start=True, stop=True)
+                    else:
+                        nc.tensor.matmul(out=y[:, r, :], lhsT=f_tile(h, 0, r), rhs=th[:, P:2 * P], start=True, stop=False)
+                        nc.tensor.matmul(out=y[:, r, :], lhsT=f_tile(h, 1, r), rhs=th[:, 0:P], start=False, stop=True)
+                return y
+
+            def first_tap(h, hi, y, ft, acc):
                 nc.vector.scalar_tensor_tensor(
                     out=acc[:, hi * 512:(hi + 1) * 512].rearrange("p (q r) -> p q r", r=4),
                     in0=ft[:, PAD - 1 + hi * 512:PAD - 1 + (hi + 1) * 512].rearrange("p (q r) -> p q r", r=4),
-                    scalar=cp[:, 0, ct:ct + 1],
-                    in1=yp[:].rearrange("p r q -> p q r"),
+                    scalar=cph[:, 0, h:h + 1],
+                    in1=y[:].rearrange("p r q -> p q r"),
                     op0=ALU.mult,
                     op1=ALU.add,
                 )
 
-            def tap1(ct, ft, acc, i):
-                (o, coef, j) = vtaps[i]
-                nc.vector.scalar_tensor_tensor(out=acc[:], in0=ft[:, PAD - o:PAD - o + N], scalar=coef[:, j, ct:ct + 1], in1=acc[:], op0=ALU.mult, op1=ALU.add)
+            def tap1(tabs, col, ft, acc, i):
+                (o, w, j) = vtaps[i]
+                nc.vector.scalar_tensor_tensor(out=acc[:, 0:N], in0=ft[:, PAD - o:PAD - o + N], scalar=tabs[w][:, j, col:col + 1], in1=acc[:, 0:N], op0=ALU.mult, op1=ALU.add)
 
-            def close1(ct, b, acc, split):
-                nc.sync.dma_start(out=out_0[b, ct * P:(ct + 1) * P, :], in_=acc[:])
+            def close_head(t, h2):
+                ct = t[0]
+                h = 2 * ct + h2
+                acc = t[3][h2]
+                for s in range(B):
+                    nc.sync.dma_start(out=out_0[(s + h) % 2, h * HD:(h + 1) * HD, :], in_=acc[s * HD:(s + 1) * HD, 0:N])
+                am = small.tile([P, 1], F32, name="am", tag="am")
+                nc.vector.tensor_reduce(out=am[:], in_=acc[:, 0:N], axis=AX.X, op=ALU.max, apply_absolute_value=True)
+                rc = small.tile([P, 1], F32, name="rc", tag="rc")
+                nc.vector.reciprocal(out=rc[:], in_=am[:])
+                nc.vector.tensor_scalar(out=acc[:, N:N + 1], in0=rc[:], scalar1=448.0, scalar2=None, op0=ALU.mult)
+                if h2 == 0:
+                    o8a = back.tile([P, N], FP8, name="o8a", tag="o8", bufs=4)
+                    nat = back.tile([P, N + 1], F32, name="nat", tag="nat", bufs=NATB)
+                    t[4]["o8a"] = o8a
+                    t[4]["nat"] = nat
+                o8a = t[4]["o8a"]
+                nat = t[4]["nat"]
+                lane = slice(h2 * HD, (h2 + 1) * HD)
+                other = slice((1 - h2) * HD, (2 - h2) * HD)
+                nc.sync.dma_start(out=nat[lane, :], in_=acc[other, :])
+                nc.scalar.activation(out=o8a[lane, :], in_=acc[lane, 0:N], func=ACT.Identity, bias=zero[lane, 0:1], scale=acc[lane, N:N + 1], saturate=False)
+                if h2 == 1:
+                    nc.sync.dma_start(out=out_1[0, ct * P:(ct + 1) * P, :], in_=o8a[:].bitcast(U8))
+                    o8b = back.tile([P, N], FP8, name="o8b", tag="o8", bufs=4)
+                    nc.scalar.activation(out=o8b[:], in_=nat[:, 0:N], func=ACT.Identity, bias=zero[:, 0:1], scale=nat[:, N:N + 1], saturate=False)
+                    nc.sync.dma_start(out=out_1[1, ct * P:(ct + 1) * P, :], in_=o8b[:].bitcast(U8))
+
+            def held_toeplitz(h2, hi, yts):
+                h = 2 * HELD + h2
+                cols = slice(h2 * HD, (h2 + 1) * HD)
+                th = ttq[h // 4][:, h % 4, :]
+                yt = psum.tile([P, B, 4, HD], F32, name="yt", tag="yt", bufs=YTB)
+                if hi == 0:
+                    nc.tensor.matmul(out=yt[:], lhsT=th[:, 0:P], rhs=fh5[:, :, 0, :, cols], start=True, stop=True)
+                else:
+                    nc.tensor.matmul(out=yt[:], lhsT=th[:, 0:P], rhs=fh5[:, :, 1, :, cols], start=True, stop=False)
+                    nc.tensor.matmul(out=yt[:], lhsT=th[:, P:2 * P], rhs=fh5[:, :, 0, :, cols], start=False, stop=True)
+                nc.scalar.copy(out=yts[:, :, hi * 4:(hi + 1) * 4, cols], in_=yt[:])
+
+            def held_turn_f(b, hi, ft):
+                tp = psum.tile([P, 4, P], F32, name="tp", tag="tp", bufs=TPB)
+                for r in range(4):
+                    nc.tensor.transpose(tp[:, r, :], f_held[:, (b * 2 + hi) * 4 + r, :], ident[:])
+                nc.scalar.copy(
+                    out=ft[:, PAD + hi * 512:PAD + (hi + 1) * 512].rearrange("p (q r) -> p q r", r=4),
+                    in_=tp[:].rearrange("p r q -> p q r"),
+                )
+
+            def held_turn_y(b, hi, yts, acc):
+                yp = psum.tile([P, 4, P], F32, name="yp", tag="yt", bufs=YTB)
+                for r in range(4):
+                    nc.tensor.transpose(yp[:, r, :], yts[:, b, hi * 4 + r, :], ident[:])
+                part = acc[:, hi * 512:(hi + 1) * 512].rearrange("p (q r) -> p q r", r=4)
+                nc.vector.tensor_tensor(out=part, in0=part, in1=yp[:].rearrange("p r q -> p q r"), op=ALU.add)
+
+            def held_close(b, acc, split):
+                nc.sync.dma_start(out=out_0[b, HELD * P:(HELD + 1) * P, :], in_=acc[:])
                 am = small.tile([P, 1], F32, name="am", tag="am")
                 nc.vector.tensor_reduce(out=am[:], in_=acc[:], axis=AX.X, op=ALU.max, apply_absolute_value=True)
                 rc = small.tile([P, 1], F32, name="rc", tag="rc")
@@ -330,63 +388,50 @@ def tile_causalwaveletfieldattentionbyte_pa_kernel(tc, x, k_w, k_b, v_w, v_b, sc
                 nc.scalar.activation(out=o8[:, 0:cut], in_=acc[:, 0:cut], func=ACT.Identity, bias=zero[:, 0:1], scale=rs[:, 0:1], saturate=False)
                 if split:
                     nc.vector.tensor_scalar(out=o8[:, cut:N], in0=acc[:, cut:N], scalar1=rs[:, 0:1], scalar2=None, op0=ALU.mult, saturate=False)
-                nc.sync.dma_start(out=out_1[b, ct * P:(ct + 1) * P, :], in_=o8[:].bitcast(U8))
+                nc.sync.dma_start(out=out_1[b, HELD * P:(HELD + 1) * P, :], in_=o8[:].bitcast(U8))
 
-            def fin_tile(t, b, part):
+            def fin_tile(t, i2, part):
                 ct = t[0]
-                g = GZ if ct >= GFIRST else 0
-                steps = []
-                for i in range(3 - g):
-                    if ct != HELD:
-                        steps.append(("tap", i))
-                if g > 0:
-                    steps.append(("z", 0))
-                steps.append(("close", 0))
-                half = (len(steps) + 1) // 2
-                for (what, i) in (steps[:half] if part == 0 else steps[half:]):
-                    if what == "tap":
-                        tap1(ct, t[2][b], t[3][b], i)
-                    elif what == "z":
-                        nc.vector.tensor_tensor(out=t[3][b][:], in0=t[3][b][:], in1=t[4][b][:], op=ALU.add)
-                    else:
-                        close1(ct, b, t[3][b], ct == HELD and b == 1)
+                if ct == HELD:
+                    if part == 0:
+                        held_close(i2, t[3][i2], i2 == 1)
+                    return
+                if part == 0:
+                    tap1((cph, cqh), 2 * ct + i2, t[2][i2], t[3][i2], 0)
+                    tap1((cph, cqh), 2 * ct + i2, t[2][i2], t[3][i2], 1)
+                else:
+                    tap1((cph, cqh), 2 * ct + i2, t[2][i2], t[3][i2], 2)
+                    close_head(t, i2)
 
             def start_pair(ct, place):
-                yts = back.tile([P, B, 8, P], F32, name="yts", tag="yts", bufs=2)
                 if ct == HELD:
-                    return (ct, yts, held_fts, held_accs, [])
+                    yts = back.tile([P, B, 8, P], F32, name="yts", tag="yts", bufs=1)
+                    return (ct, yts, held_fts, held_accs, {})
                 accs = []
-                for b in range(B):
-                    acc = back.tile([P, N], F32, name="acc", tag="acc", bufs=5)
+                for i2 in range(2):
+                    acc = back.tile([P, N + 1], F32, name="acc", tag="acc", bufs=5)
                     accs.append(acc)
-                return (ct, yts, (ft_bufs[(2 * place) % 6], ft_bufs[(2 * place + 1) % 6]), accs, [])
+                return (ct, {}, (ft_bufs[(2 * place) % 6], ft_bufs[(2 * place + 1) % 6]), accs, {})
 
-            def gz_sum(ct, fts):
-                zs = []
-                for b in range(B):
-                    z = back.tile([P, N], F32, name="z", tag="z", bufs=3)
-                    for i in range(3 - GZ, 3):
-                        (o, coef, j) = vtaps[i]
-                        dst = z
-                        if i > 3 - GZ:
-                            dst = back.tile([P, N], F32, name="zt", tag="zt", bufs=1)
-                        nc.gpsimd.tensor_scalar(out=dst[:], in0=fts[b][:, PAD - o:PAD - o + N], scalar1=coef[:, j, ct:ct + 1], scalar2=0.0, op0=ALU.mult, op1=ALU.add)
-                        if i > 3 - GZ:
-                            nc.gpsimd.tensor_tensor(out=z[:], in0=z[:], in1=dst[:], op=ALU.add)
-                    zs.append(z)
-                return zs
+            def empty(t, i2, hi):
+                if t[0] == HELD:
+                    held_turn_y(i2, hi, t[1], t[3][i2])
+                else:
+                    first_tap(2 * t[0] + i2, hi, t[1][(i2, hi)], t[2][i2], t[3][i2])
 
             def weave(cur, nxt, units, tp_tag):
                 for k in range(4):
                     k1, k0 = divmod(k, 2)
                     if k < 2 and cur is not None:
-                        turn_y(cur[0], k0, 1, cur[1], cur[2][k0], cur[3][k0])
+                        empty(cur, k0, 1)
                     if k >= 2 and nxt is not None:
-                        turn_y(nxt[0], k0, 0, nxt[1], nxt[2][k0], nxt[3][k0])
+                        empty(nxt, k0, 0)
                     if nxt is not None:
                         if nxt[0] != HELD:
-                            turn_f(nxt[0], k0, k1, nxt[2][k0], tp_tag)
-                        toeplitz(nxt[0], k0, k1, nxt[1])
+                            turn_f(2 * nxt[0] + k0, k1, nxt[2][k0], tp_tag)
+                            nxt[1][(k0, k1)] = toep(2 * nxt[0] + k0, k1)
+                        else:
+                            held_toeplitz(k0, k1, nxt[1])
                     per = len(units) // 4
                     run(units[per * k:per * (k + 1)])
                     if cur is not None:
@@ -406,12 +451,12 @@ def tile_causalwaveletfieldattentionbyte_pa_kernel(tc, x, k_w, k_b, v_w, v_b, sc
                 held_accs.append(hacc)
             for k in range(4):
                 k1, k0 = divmod(k, 2)
-                turn_f(HELD, k0, k1, held_fts[k0], "tp")
+                held_turn_f(k0, k1, held_fts[k0])
             for b in range(B):
                 nc.vector.tensor_scalar(out=held_accs[b][:], in0=held_fts[b][:, PAD - 1:PAD - 1 + N], scalar1=cp[:, 0, HELD:HELD + 1], scalar2=None, op0=ALU.mult)
             for i in range(3):
                 for b in range(B):
-                    tap1(HELD, held_fts[b], held_accs[b], i)
+                    tap1((cp, cq), HELD, held_fts[b], held_accs[b], i)
             order = [ct for ct in range(NCT) if ct != HELD] + [HELD]
             shares = (16, 8, 8, 8, 8)
             cur = None

@@ -263,11 +263,11 @@ def tile_causalwaveletfieldattentionbyte_pa_kernel(tc, x, k_w, k_b, v_w, v_b, sc
             run(front_units(0, 0))
             prep(raw_x[2], x_codes, x_sc, 1024)
             run(front_units(1, 0))
-            prep(raw_x[3], x_codes, x_sc, 1536, True)
+            prep(raw_x[3], x_codes, x_sc, 1536)
             run(front_units(2, 0))
-            prep(raw_kw1, kw_codes, kw_sc, 512, True)
+            prep(raw_kw1, kw_codes, kw_sc, 512)
             run(front_units(3, 0))
-            prep(raw_vw1, vw_codes, vw_sc, 512, True)
+            prep(raw_vw1, vw_codes, vw_sc, 512)
 
         PAD = 8
         vtaps = ((2, 0, 1), (3, 1, 0), (6, 1, 1))
@@ -328,8 +328,8 @@ def tile_causalwaveletfieldattentionbyte_pa_kernel(tc, x, k_w, k_b, v_w, v_b, sc
                 am = small.tile([P, 1], F32, name="am", tag="am")
                 nc.vector.tensor_reduce(out=am[:], in_=acc[:, 0:N], axis=AX.X, op=ALU.max, apply_absolute_value=True)
                 rc = small.tile([P, 1], F32, name="rc", tag="rc")
-                nc.vector.reciprocal(out=rc[:], in_=am[:])
-                nc.vector.tensor_scalar(out=acc[:, N:N + 1], in0=rc[:], scalar1=448.0, scalar2=None, op0=ALU.mult)
+                nc.scalar.activation(out=rc[:], in_=am[:], func=ACT.Copy, scale=1.0 / 448.0)
+                nc.vector.reciprocal(out=acc[:, N:N + 1], in_=rc[:])
                 if h2 == 0:
                     o8a = back.tile([P, N], FP8, name="o8a", tag="o8", bufs=4)
                     nat = back.tile([P, N + 1], F32, name="nat", tag="nat", bufs=NATB)
@@ -453,7 +453,7 @@ def tile_causalwaveletfieldattentionbyte_pa_kernel(tc, x, k_w, k_b, v_w, v_b, sc
                 k1, k0 = divmod(k, 2)
                 held_turn_f(k0, k1, held_fts[k0])
             for b in range(B):
-                nc.vector.tensor_scalar(out=held_accs[b][:], in0=held_fts[b][:, PAD - 1:PAD - 1 + N], scalar1=cp[:, 0, HELD:HELD + 1], scalar2=None, op0=ALU.mult)
+                nc.scalar.activation(out=held_accs[b][:], in_=held_fts[b][:, PAD - 1:PAD - 1 + N], func=ACT.Copy, scale=cp[:, 0, HELD:HELD + 1])
             for i in range(3):
                 for b in range(B):
                     tap1((cp, cq), HELD, held_fts[b], held_accs[b], i)

@@ -24,6 +24,8 @@ MXB = 2
 TPB = 1
 YTB = 5
 HELD = 1
+NAT = (1, 7)
+FH = tuple(h for h in range(H) if h // 2 not in NAT)
 NATB = 3
 NPASS = D // 512
 NCT = C // P
@@ -99,8 +101,11 @@ def tile_causalwaveletfieldattentionbyte_pa_kernel(tc, x, k_w, k_b, v_w, v_b, sc
         vw_codes = keep.tile([P, NPASS, C], U32, name="vw_codes", tag="vw_codes", align_bytes=64)
         vw_sc = keep.tile([P, NPASS, C], U8, name="vw_sc", tag="vw_sc", align_bytes=64)
         m_sb = keep.tile([P, NTG * 4, H], F32, name="m_sb", tag="m_sb")
-        f_sb = keep.tile([P, 8, H, B, HD], F32, name="f_sb", tag="f_sb")
-        f_held = keep.tile([P, NTG * 4, P], F32, name="f_held", tag="f_held")
+        f_sb = keep.tile([P, 8, len(FH), B, HD], F32, name="f_sb", tag="f_sb")
+        f_nat = {}
+        for ct in NAT:
+            fn = keep.tile([P, NTG * 4, P], F32, name="f_nat%d" % ct, tag="f_nat%d" % ct)
+            f_nat[ct] = fn
         taps_of = {1: ((1, T1),)}
         for j in range(2, NS):
             dq = 2 ** (j - 2)
@@ -183,10 +188,10 @@ def tile_causalwaveletfieldattentionbyte_pa_kernel(tc, x, k_w, k_b, v_w, v_b, sc
             nc.scalar.activation(out=m_sb[:, tau, qu * 4:(qu + 1) * 4], in_=msq[:], func=ACT.Sqrt)
             for h4 in range(4):
                 h = qu * 4 + h4
-                if h // 2 == HELD:
-                    dst = f_held[:, tau, (h % 2) * HD:(h % 2 + 1) * HD]
+                if h // 2 in NAT:
+                    dst = f_nat[h // 2][:, tau, (h % 2) * HD:(h % 2 + 1) * HD]
                 else:
-                    dst = f_sb[:, tau % 8, h, (tau // 8 + h) % 2, :]
+                    dst = f_sb[:, tau % 8, FH.index(h), (tau // 8 + h) % 2, :]
                 nc.scalar.activation(
                     out=dst,
                     in_=kvt[:, 1, h4 * HD:(h4 + 1) * HD],
@@ -280,10 +285,9 @@ def tile_causalwaveletfieldattentionbyte_pa_kernel(tc, x, k_w, k_b, v_w, v_b, sc
                 ftb = back.tile([P, PAD + N], F32, name="ft%d" % i, tag="ft%d" % i, bufs=1)
                 nc.gpsimd.memset(ftb[:, 0:PAD], 0.0)
                 ft_bufs.append(ftb)
-            fh5 = f_held[:].rearrange("p (b a r) c -> p b a r c", b=B, a=2)
 
             def f_tile(h, hi, r):
-                return f_sb[:, hi * 4 + r, h].rearrange("p s c -> p (s c)")
+                return f_sb[:, hi * 4 + r, FH.index(h)].rearrange("p s c -> p (s c)")
 
             def turn_f(h, hi, ft, tag):
                 tp = psum.tile([P, 4, P], F32, name="tp", tag=tag, bufs=(TPB if tag == "tp" else MXB))
@@ -347,38 +351,49 @@ def tile_causalwaveletfieldattentionbyte_pa_kernel(tc, x, k_w, k_b, v_w, v_b, sc
                     nc.scalar.activation(out=o8b[:], in_=nat[:, 0:N], func=ACT.Identity, bias=zero[:, 0:1], scale=nat[:, N:N + 1], saturate=False)
                     nc.sync.dma_start(out=out_1[1, ct * P:(ct + 1) * P, :], in_=o8b[:].bitcast(U8))
 
-            def held_toeplitz(h2, hi, yts):
-                h = 2 * HELD + h2
+            def nat_toeplitz(ct, h2, hi, yts):
+                h = 2 * ct + h2
                 cols = slice(h2 * HD, (h2 + 1) * HD)
                 th = ttq[h // 4][:, h % 4, :]
+                fn5 = f_nat[ct][:].rearrange("p (b a r) c -> p b a r c", b=B, a=2)
                 yt = psum.tile([P, B, 4, HD], F32, name="yt", tag="yt", bufs=YTB)
                 if hi == 0:
-                    nc.tensor.matmul(out=yt[:], lhsT=th[:, 0:P], rhs=fh5[:, :, 0, :, cols], start=True, stop=True)
+                    nc.tensor.matmul(out=yt[:], lhsT=th[:, 0:P], rhs=fn5[:, :, 0, :, cols], start=True, stop=True)
                 else:
-                    nc.tensor.matmul(out=yt[:], lhsT=th[:, 0:P], rhs=fh5[:, :, 1, :, cols], start=True, stop=False)
-                    nc.tensor.matmul(out=yt[:], lhsT=th[:, P:2 * P], rhs=fh5[:, :, 0, :, cols], start=False, stop=True)
+                    nc.tensor.matmul(out=yt[:], lhsT=th[:, 0:P], rhs=fn5[:, :, 1, :, cols], start=True, stop=False)
+                    nc.tensor.matmul(out=yt[:], lhsT=th[:, P:2 * P], rhs=fn5[:, :, 0, :, cols], start=False, stop=True)
                 nc.scalar.copy(out=yts[:, :, hi * 4:(hi + 1) * 4, cols], in_=yt[:])
 
-            def held_turn_f(b, hi, ft):
-                tp = psum.tile([P, 4, P], F32, name="tp", tag="tp", bufs=TPB)
+            def nat_turn_f(ct, b, hi, ft, tag):
+                tp = psum.tile([P, 4, P], F32, name="tp", tag=tag, bufs=(TPB if tag == "tp" else MXB))
                 for r in range(4):
-                    nc.tensor.transpose(tp[:, r, :], f_held[:, (b * 2 + hi) * 4 + r, :], ident[:])
+                    nc.tensor.transpose(tp[:, r, :], f_nat[ct][:, (b * 2 + hi) * 4 + r, :], ident[:])
                 nc.scalar.copy(
                     out=ft[:, PAD + hi * 512:PAD + (hi + 1) * 512].rearrange("p (q r) -> p q r", r=4),
                     in_=tp[:].rearrange("p r q -> p q r"),
                 )
 
-            def held_turn_y(b, hi, yts, acc):
+            def nat_turn_y(ct, b, hi, yts, ft, acc):
                 yp = psum.tile([P, 4, P], F32, name="yp", tag="yt", bufs=YTB)
                 for r in range(4):
                     nc.tensor.transpose(yp[:, r, :], yts[:, b, hi * 4 + r, :], ident[:])
                 part = acc[:, hi * 512:(hi + 1) * 512].rearrange("p (q r) -> p q r", r=4)
-                nc.vector.tensor_tensor(out=part, in0=part, in1=yp[:].rearrange("p r q -> p q r"), op=ALU.add)
+                if ct == HELD:
+                    nc.vector.tensor_tensor(out=part, in0=part, in1=yp[:].rearrange("p r q -> p q r"), op=ALU.add)
+                    return
+                nc.vector.scalar_tensor_tensor(
+                    out=part,
+                    in0=ft[:, PAD - 1 + hi * 512:PAD - 1 + (hi + 1) * 512].rearrange("p (q r) -> p q r", r=4),
+                    scalar=cp[:, 0, ct:ct + 1],
+                    in1=yp[:].rearrange("p r q -> p q r"),
+                    op0=ALU.mult,
+                    op1=ALU.add,
+                )
 
-            def held_close(b, acc, split):
-                nc.sync.dma_start(out=out_0[b, HELD * P:(HELD + 1) * P, :], in_=acc[:])
+            def nat_close(ct, b, acc, split):
+                nc.sync.dma_start(out=out_0[b, ct * P:(ct + 1) * P, :], in_=acc[:, 0:N])
                 am = small.tile([P, 1], F32, name="am", tag="am")
-                nc.vector.tensor_reduce(out=am[:], in_=acc[:], axis=AX.X, op=ALU.max, apply_absolute_value=True)
+                nc.vector.tensor_reduce(out=am[:], in_=acc[:, 0:N], axis=AX.X, op=ALU.max, apply_absolute_value=True)
                 rc = small.tile([P, 1], F32, name="rc", tag="rc")
                 nc.vector.reciprocal(out=rc[:], in_=am[:])
                 rs = small.tile([P, 1], F32, name="rs", tag="rs")
@@ -388,34 +403,41 @@ def tile_causalwaveletfieldattentionbyte_pa_kernel(tc, x, k_w, k_b, v_w, v_b, sc
                 nc.scalar.activation(out=o8[:, 0:cut], in_=acc[:, 0:cut], func=ACT.Identity, bias=zero[:, 0:1], scale=rs[:, 0:1], saturate=False)
                 if split:
                     nc.vector.tensor_scalar(out=o8[:, cut:N], in0=acc[:, cut:N], scalar1=rs[:, 0:1], scalar2=None, op0=ALU.mult, saturate=False)
-                nc.sync.dma_start(out=out_1[b, HELD * P:(HELD + 1) * P, :], in_=o8[:].bitcast(U8))
+                nc.sync.dma_start(out=out_1[b, ct * P:(ct + 1) * P, :], in_=o8[:].bitcast(U8))
 
             def fin_tile(t, i2, part):
                 ct = t[0]
                 if ct == HELD:
                     if part == 0:
-                        held_close(i2, t[3][i2], i2 == 1)
+                        nat_close(ct, i2, t[3][i2], i2 == 1)
                     return
+                tabs = (cp, cq) if ct in NAT else (cph, cqh)
+                col = ct if ct in NAT else 2 * ct + i2
                 if part == 0:
-                    tap1((cph, cqh), 2 * ct + i2, t[2][i2], t[3][i2], 0)
-                    tap1((cph, cqh), 2 * ct + i2, t[2][i2], t[3][i2], 1)
+                    tap1(tabs, col, t[2][i2], t[3][i2], 0)
+                    tap1(tabs, col, t[2][i2], t[3][i2], 1)
                 else:
-                    tap1((cph, cqh), 2 * ct + i2, t[2][i2], t[3][i2], 2)
-                    close_head(t, i2)
+                    tap1(tabs, col, t[2][i2], t[3][i2], 2)
+                    if ct in NAT:
+                        nat_close(ct, i2, t[3][i2], False)
+                    else:
+                        close_head(t, i2)
 
             def start_pair(ct, place):
+                prod = {}
+                if ct in NAT:
+                    prod = back.tile([P, B, 8, P], F32, name="yts", tag="yts", bufs=2)
                 if ct == HELD:
-                    yts = back.tile([P, B, 8, P], F32, name="yts", tag="yts", bufs=1)
-                    return (ct, yts, held_fts, held_accs, {})
+                    return (ct, prod, held_fts, held_accs, {})
                 accs = []
                 for i2 in range(2):
                     acc = back.tile([P, N + 1], F32, name="acc", tag="acc", bufs=5)
                     accs.append(acc)
-                return (ct, {}, (ft_bufs[(2 * place) % 6], ft_bufs[(2 * place + 1) % 6]), accs, {})
+                return (ct, prod, (ft_bufs[(2 * place) % 6], ft_bufs[(2 * place + 1) % 6]), accs, {})
 
             def empty(t, i2, hi):
-                if t[0] == HELD:
-                    held_turn_y(i2, hi, t[1], t[3][i2])
+                if t[0] in NAT:
+                    nat_turn_y(t[0], i2, hi, t[1], t[2][i2], t[3][i2])
                 else:
                     first_tap(2 * t[0] + i2, hi, t[1][(i2, hi)], t[2][i2], t[3][i2])
 
@@ -427,11 +449,13 @@ def tile_causalwaveletfieldattentionbyte_pa_kernel(tc, x, k_w, k_b, v_w, v_b, sc
                     if k >= 2 and nxt is not None:
                         empty(nxt, k0, 0)
                     if nxt is not None:
-                        if nxt[0] != HELD:
+                        if nxt[0] not in NAT:
                             turn_f(2 * nxt[0] + k0, k1, nxt[2][k0], tp_tag)
                             nxt[1][(k0, k1)] = toep(2 * nxt[0] + k0, k1)
                         else:
-                            held_toeplitz(k0, k1, nxt[1])
+                            if nxt[0] != HELD:
+                                nat_turn_f(nxt[0], k0, k1, nxt[2][k0], tp_tag)
+                            nat_toeplitz(nxt[0], k0, k1, nxt[1])
                     per = len(units) // 4
                     run(units[per * k:per * (k + 1)])
                     if cur is not None:
@@ -451,7 +475,7 @@ def tile_causalwaveletfieldattentionbyte_pa_kernel(tc, x, k_w, k_b, v_w, v_b, sc
                 held_accs.append(hacc)
             for k in range(4):
                 k1, k0 = divmod(k, 2)
-                held_turn_f(k0, k1, held_fts[k0])
+                nat_turn_f(HELD, k0, k1, held_fts[k0], "tp")
             for b in range(B):
                 nc.scalar.activation(out=held_accs[b][:], in_=held_fts[b][:, PAD - 1:PAD - 1 + N], func=ACT.Copy, scale=cp[:, 0, HELD:HELD + 1])
             for i in range(3):

@@ -209,6 +209,26 @@ def tile_causalwaveletfieldattentionbyte_pa_kernel(tc, x, k_w, k_b, v_w, v_b, sc
             for (fn, arg) in pieces:
                 fn(arg)
 
+        def w_view(w, half):
+            return w[512 * half:512 * (half + 1), :].rearrange("(s j) d -> j s d", j=P)
+
+        def prep_pass(raw, codes, scales, col0, g, new_grouped):
+            grouped = new_grouped()
+            gw = grouped[:].bitcast(F32).rearrange("p (s j u) -> p s j u", s=4, u=2)
+            for a in range(2):
+                xt = psum.tile([P, 2, 2, P], F32, name="xt", tag="yt", bufs=YTB)
+                for s2 in range(2):
+                    words = raw[:, 2 * a + s2, :].bitcast(F32)
+                    for u in range(2):
+                        nc.tensor.transpose(xt[:, s2, u, :], words[:, 256 * g + u:256 * (g + 1):2], ident[:])
+                nc.scalar.copy(out=gw[:, 2 * a:2 * a + 2], in_=xt[:].rearrange("p s u j -> p s j u"))
+            nc.vector.quantize_mx(
+                out=codes[:, g, col0:col0 + 512].bitcast(FP8X4),
+                scales=scales[:, g, col0:col0 + 512],
+                in_=grouped[:],
+            )
+
+        raw_late = []
         with ExitStack() as front:
             raw_pool = front.enter_context(tc.tile_pool(name="raw", bufs=6))
             grp = front.enter_context(tc.tile_pool(name="grp", bufs=3))
@@ -218,9 +238,6 @@ def tile_causalwaveletfieldattentionbyte_pa_kernel(tc, x, k_w, k_b, v_w, v_b, sc
                 for a in range(2):
                     nc.sync.dma_start(out=t[:, 2 * a:2 * a + 2, :], in_=view[:, 2 * a:2 * a + 2, :])
                 return t
-
-            def w_view(w, half):
-                return w[512 * half:512 * (half + 1), :].rearrange("(s j) d -> j s d", j=P)
 
             def x_view(tg):
                 b, hi = divmod(tg, 2)
@@ -233,29 +250,19 @@ def tile_causalwaveletfieldattentionbyte_pa_kernel(tc, x, k_w, k_b, v_w, v_b, sc
             nc.sync.dma_start(out=kvb[:, 1, :], in_=v_b.partition_broadcast(P))
             for tg in range(1, NTG):
                 raw_x.append(load(x_view(tg), "raw_x%d" % tg))
-            raw_kw1 = load(w_view(k_w, 1), "raw_kw1")
-            raw_vw1 = load(w_view(v_w, 1), "raw_vw1")
+            for (w, nm) in ((k_w, "raw_kw1"), (v_w, "raw_vw1")):
+                rl = keep.tile([P, 4, D], BF16, name=nm, tag="yts", bufs=2)
+                for a in range(2):
+                    nc.sync.dma_start(out=rl[:, 2 * a:2 * a + 2, :], in_=w_view(w, 1)[:, 2 * a:2 * a + 2, :])
+                raw_late.append(rl)
 
-            def prep(raw, codes, scales, col0, shared=False):
+            def front_grouped():
+                grouped = grp.tile([P, 2048], BF16, name="grouped", tag="grouped", align_bytes=64)
+                return grouped
+
+            def prep(raw, codes, scales, col0):
                 for g in range(NPASS):
-                    grouped = grp.tile([P, 2048], BF16, name="grouped", tag="grouped", align_bytes=64)
-                    gw = grouped[:].bitcast(F32).rearrange("p (s j u) -> p s j u", s=4, u=2)
-                    for a in range(2):
-                        xt = psum.tile([P, 2, 2, P], F32, name="xt", tag="yt", bufs=YTB)
-                        for s2 in range(2):
-                            words = raw[:, 2 * a + s2, :].bitcast(F32)
-                            for u in range(2):
-                                nc.tensor.transpose(xt[:, s2, u, :], words[:, 256 * g + u:256 * (g + 1):2], ident[:])
-                        src = xt[:].rearrange("p s u j -> p s j u")
-                        if shared and a == 1:
-                            nc.vector.tensor_copy(out=gw[:, 2 * a:2 * a + 2], in_=src)
-                        else:
-                            nc.scalar.copy(out=gw[:, 2 * a:2 * a + 2], in_=src)
-                    nc.vector.quantize_mx(
-                        out=codes[:, g, col0:col0 + 512].bitcast(FP8X4),
-                        scales=scales[:, g, col0:col0 + 512],
-                        in_=grouped[:],
-                    )
+                    prep_pass(raw, codes, scales, col0, g, front_grouped)
 
             build_masks()
             prep(raw_kw0, kw_codes, kw_sc, 0)
@@ -270,9 +277,7 @@ def tile_causalwaveletfieldattentionbyte_pa_kernel(tc, x, k_w, k_b, v_w, v_b, sc
             run(front_units(1, 0))
             prep(raw_x[3], x_codes, x_sc, 1536)
             run(front_units(2, 0))
-            prep(raw_kw1, kw_codes, kw_sc, 512)
             run(front_units(3, 0))
-            prep(raw_vw1, vw_codes, vw_sc, 512)
 
         PAD = 8
         vtaps = ((2, 0, 1), (3, 1, 0), (6, 1, 1))
@@ -285,6 +290,13 @@ def tile_causalwaveletfieldattentionbyte_pa_kernel(tc, x, k_w, k_b, v_w, v_b, sc
                 ftb = back.tile([P, PAD + N], F32, name="ft%d" % i, tag="ft%d" % i, bufs=1)
                 nc.gpsimd.memset(ftb[:, 0:PAD], 0.0)
                 ft_bufs.append(ftb)
+
+            def late_grouped():
+                grouped = back.tile([P, 2048], BF16, name="grouped2", tag="nat", bufs=NATB, align_bytes=64)
+                return grouped
+
+            def late_prep(i):
+                prep_pass(raw_late[i // 2], (kw_codes, vw_codes)[i // 2], (kw_sc, vw_sc)[i // 2], 512, i % 2, late_grouped)
 
             def f_tile(h, hi, r):
                 return f_sb[:, hi * 4 + r, FH.index(h)].rearrange("p s c -> p (s c)")
@@ -336,7 +348,7 @@ def tile_causalwaveletfieldattentionbyte_pa_kernel(tc, x, k_w, k_b, v_w, v_b, sc
                 nc.vector.reciprocal(out=acc[:, N:N + 1], in_=rc[:])
                 if h2 == 0:
                     o8a = back.tile([P, N], FP8, name="o8a", tag="o8", bufs=4)
-                    nat = back.tile([P, N + 1], F32, name="nat", tag="nat", bufs=NATB)
+                    nat = back.tile([P, N + 1], F32, name="nat", tag="nat", bufs=NATB, align_bytes=64)
                     t[4]["o8a"] = o8a
                     t[4]["nat"] = nat
                 o8a = t[4]["o8a"]
@@ -426,7 +438,7 @@ def tile_causalwaveletfieldattentionbyte_pa_kernel(tc, x, k_w, k_b, v_w, v_b, sc
             def start_pair(ct, place):
                 prod = {}
                 if ct in NAT:
-                    prod = back.tile([P, B, 8, P], F32, name="yts", tag="yts", bufs=2)
+                    prod = keep.tile([P, B, 8, P], F32, name="yts", tag="yts", bufs=2)
                 if ct == HELD:
                     return (ct, prod, held_fts, held_accs, {})
                 accs = []
@@ -488,5 +500,11 @@ def tile_causalwaveletfieldattentionbyte_pa_kernel(tc, x, k_w, k_b, v_w, v_b, sc
                 nxt = start_pair(order[pos], pos + 1) if pos < NCT else None
                 first = sum(shares[:pos])
                 units = late[first:first + shares[pos]] if pos < len(shares) else []
+                if pos == 0:
+                    woven = []
+                    for k in range(4):
+                        woven.extend(units[4 * k:4 * k + 4])
+                        woven.append((late_prep, k))
+                    units = woven
                 weave(cur, nxt, units, "tp" if pos < len(shares) else "mx")
                 cur = nxt

@@ -339,8 +339,7 @@ def tile_causalwaveletfieldattentionbyte_pa_kernel(tc, x, k_w, k_b, v_w, v_b, sc
                 ct = t[0]
                 h = 2 * ct + h2
                 acc = t[3][h2]
-                for s in range(B):
-                    nc.sync.dma_start(out=out_0[(s + h) % 2, h * HD:(h + 1) * HD, :], in_=acc[s * HD:(s + 1) * HD, 0:N])
+                nc.sync.dma_start(out=out_0[0, h * HD:(h + 1) * HD, :], in_=acc[h2 * HD:(h2 + 1) * HD, 0:N])
                 am = small.tile([P, 1], F32, name="am", tag="am")
                 nc.vector.tensor_reduce(out=am[:], in_=acc[:, 0:N], axis=AX.X, op=ALU.max, apply_absolute_value=True)
                 rc = small.tile([P, 1], F32, name="rc", tag="rc")
@@ -359,6 +358,7 @@ def tile_causalwaveletfieldattentionbyte_pa_kernel(tc, x, k_w, k_b, v_w, v_b, sc
                 nc.scalar.activation(out=o8a[lane, :], in_=acc[lane, 0:N], func=ACT.Identity, bias=zero[lane, 0:1], scale=acc[lane, N:N + 1], saturate=False)
                 if h2 == 1:
                     nc.sync.dma_start(out=out_1[0, ct * P:(ct + 1) * P, :], in_=o8a[:].bitcast(U8))
+                    nc.sync.dma_start(out=out_0[1, ct * P:(ct + 1) * P, :], in_=nat[:, 0:N])
                     o8b = back.tile([P, N], FP8, name="o8b", tag="o8", bufs=4)
                     nc.scalar.activation(out=o8b[:], in_=nat[:, 0:N], func=ACT.Identity, bias=zero[:, 0:1], scale=nat[:, N:N + 1], saturate=False)
                     nc.sync.dma_start(out=out_1[1, ct * P:(ct + 1) * P, :], in_=o8b[:].bitcast(U8))
@@ -411,9 +411,10 @@ def tile_causalwaveletfieldattentionbyte_pa_kernel(tc, x, k_w, k_b, v_w, v_b, sc
                 rs = small.tile([P, 1], F32, name="rs", tag="rs")
                 nc.vector.tensor_scalar(out=rs[:], in0=rc[:], scalar1=448.0, scalar2=None, op0=ALU.mult)
                 o8 = back.tile([P, N], FP8, name="o8", tag="o8", bufs=4)
-                cut = N // 2 if split else N
-                nc.scalar.activation(out=o8[:, 0:cut], in_=acc[:, 0:cut], func=ACT.Identity, bias=zero[:, 0:1], scale=rs[:, 0:1], saturate=False)
-                if split:
+                cut = (N, N // 2, 0)[split]
+                if cut > 0:
+                    nc.scalar.activation(out=o8[:, 0:cut], in_=acc[:, 0:cut], func=ACT.Identity, bias=zero[:, 0:1], scale=rs[:, 0:1], saturate=False)
+                if cut < N:
                     nc.vector.tensor_scalar(out=o8[:, cut:N], in0=acc[:, cut:N], scalar1=rs[:, 0:1], scalar2=None, op0=ALU.mult, saturate=False)
                 nc.sync.dma_start(out=out_1[b, ct * P:(ct + 1) * P, :], in_=o8[:].bitcast(U8))
 
@@ -421,7 +422,7 @@ def tile_causalwaveletfieldattentionbyte_pa_kernel(tc, x, k_w, k_b, v_w, v_b, sc
                 ct = t[0]
                 if ct == HELD:
                     if part == 0:
-                        nat_close(ct, i2, t[3][i2], i2 == 1)
+                        nat_close(ct, i2, t[3][i2], 1 + i2)
                     return
                 tabs = (cp, cq) if ct in NAT else (cph, cqh)
                 col = ct if ct in NAT else 2 * ct + i2
@@ -431,7 +432,7 @@ def tile_causalwaveletfieldattentionbyte_pa_kernel(tc, x, k_w, k_b, v_w, v_b, sc
                 else:
                     tap1(tabs, col, t[2][i2], t[3][i2], 2)
                     if ct in NAT:
-                        nat_close(ct, i2, t[3][i2], False)
+                        nat_close(ct, i2, t[3][i2], 0)
                     else:
                         close_head(t, i2)
 

@@ -20,9 +20,9 @@ ACT = mybir.ActivationFunctionType
 AX = mybir.AxisListType
 
 P = 128
-MXB = 2
+MXB = 3
 TPB = 1
-YTB = 5
+YTB = 4
 HELD = 1
 NAT = (1, 7)
 FH = tuple(h for h in range(H) if h // 2 not in NAT)

@@ -310,16 +310,14 @@ def tile_causalwaveletfieldattentionbyte_pa_kernel(tc, x, k_w, k_b, v_w, v_b, sc
                     in_=tp[:].rearrange("p r q -> p q r"),
                 )
 
-            def toep(h, hi):
+            def toep(h, hi, y, phases):
                 th = ttq[h // 4][:, h % 4, :]
-                y = psum.tile([P, 4, P], F32, name="y", tag="yt", bufs=YTB)
-                for r in range(4):
+                for r in phases:
                     if hi == 0:
                         nc.tensor.matmul(out=y[:, r, :], lhsT=f_tile(h, 0, r), rhs=th[:, 0:P], start=True, stop=True)
                     else:
                         nc.tensor.matmul(out=y[:, r, :], lhsT=f_tile(h, 0, r), rhs=th[:, P:2 * P], start=True, stop=False)
                         nc.tensor.matmul(out=y[:, r, :], lhsT=f_tile(h, 1, r), rhs=th[:, 0:P], start=False, stop=True)
-                return y
 
             def first_tap(h, hi, y, ft, acc):
                 nc.vector.scalar_tensor_tensor(
@@ -461,16 +459,21 @@ def tile_causalwaveletfieldattentionbyte_pa_kernel(tc, x, k_w, k_b, v_w, v_b, sc
                         empty(cur, k0, 1)
                     if k >= 2 and nxt is not None:
                         empty(nxt, k0, 0)
+                    y = None
                     if nxt is not None:
                         if nxt[0] not in NAT:
                             turn_f(2 * nxt[0] + k0, k1, nxt[2][k0], tp_tag)
-                            nxt[1][(k0, k1)] = toep(2 * nxt[0] + k0, k1)
+                            y = psum.tile([P, 4, P], F32, name="y", tag="yt", bufs=YTB)
+                            nxt[1][(k0, k1)] = y
+                            toep(2 * nxt[0] + k0, k1, y, (0, 1))
                         else:
                             if nxt[0] != HELD:
                                 nat_turn_f(nxt[0], k0, k1, nxt[2][k0], tp_tag)
                             nat_toeplitz(nxt[0], k0, k1, nxt[1])
                     per = len(units) // 4
                     run(units[per * k:per * (k + 1)])
+                    if y is not None:
+                        toep(2 * nxt[0] + k0, k1, y, (2, 3))
                     if cur is not None:
                         if k in (0, 1):
                             fin_tile(cur, 0, k)

@@ -341,8 +341,8 @@ def tile_causalwaveletfieldattentionbyte_pa_kernel(tc, x, k_w, k_b, v_w, v_b, sc
                 am = small.tile([P, 1], F32, name="am", tag="am")
                 nc.vector.tensor_reduce(out=am[:], in_=acc[:, 0:N], axis=AX.X, op=ALU.max, apply_absolute_value=True)
                 rc = small.tile([P, 1], F32, name="rc", tag="rc")
-                nc.scalar.activation(out=rc[:], in_=am[:], func=ACT.Copy, scale=1.0 / 448.0)
-                nc.vector.reciprocal(out=acc[:, N:N + 1], in_=rc[:])
+                nc.vector.reciprocal(out=rc[:], in_=am[:])
+                nc.scalar.activation(out=acc[:, N:N + 1], in_=rc[:], func=ACT.Copy, scale=448.0)
                 if h2 == 0:
                     o8a = back.tile([P, N], FP8, name="o8a", tag="o8", bufs=4)
                     nat = back.tile([P, N + 1], F32, name="nat", tag="nat", bufs=NATB, align_bytes=64)

@@ -383,6 +383,8 @@ def tile_causalwaveletfieldattentionbyte_pa_kernel(tc, x, k_w, k_b, v_w, v_b, sc
                     in_=tp[:].rearrange("p r q -> p q r"),
                 )
 
+            held_am = []
+
             def nat_turn_y(ct, b, hi, yts, ft, acc):
                 yp = psum.tile([P, 4, P], F32, name="yp", tag="yt", bufs=YTB)
                 for r in range(4):
@@ -390,6 +392,9 @@ def tile_causalwaveletfieldattentionbyte_pa_kernel(tc, x, k_w, k_b, v_w, v_b, sc
                 part = acc[:, hi * 512:(hi + 1) * 512].rearrange("p (q r) -> p q r", r=4)
                 if ct == HELD:
                     nc.vector.tensor_tensor(out=part, in0=part, in1=yp[:].rearrange("p r q -> p q r"), op=ALU.add)
+                    half = slice(hi * 512, (hi + 1) * 512)
+                    nc.sync.dma_start(out=out_0[b, ct * P:(ct + 1) * P, half], in_=acc[:, half])
+                    nc.vector.tensor_reduce(out=held_am[b][:, hi:hi + 1], in_=acc[:, half], axis=AX.X, op=ALU.max, apply_absolute_value=True)
                     return
                 nc.vector.scalar_tensor_tensor(
                     out=part,
@@ -401,13 +406,17 @@ def tile_causalwaveletfieldattentionbyte_pa_kernel(tc, x, k_w, k_b, v_w, v_b, sc
                 )
 
             def nat_close(ct, b, acc, split):
-                nc.sync.dma_start(out=out_0[b, ct * P:(ct + 1) * P, :], in_=acc[:, 0:N])
-                am = small.tile([P, 1], F32, name="am", tag="am")
-                nc.vector.tensor_reduce(out=am[:], in_=acc[:, 0:N], axis=AX.X, op=ALU.max, apply_absolute_value=True)
                 rc = small.tile([P, 1], F32, name="rc", tag="rc")
-                nc.vector.reciprocal(out=rc[:], in_=am[:])
                 rs = small.tile([P, 1], F32, name="rs", tag="rs")
-                nc.vector.tensor_scalar(out=rs[:], in0=rc[:], scalar1=448.0, scalar2=None, op0=ALU.mult)
+                if ct == HELD:
+                    nc.vector.tensor_scalar(out=rc[:], in0=held_am[b][:, 0:1], scalar1=held_am[b][:, 1:2], scalar2=1.0 / 448.0, op0=ALU.max, op1=ALU.mult)
+                    nc.vector.reciprocal(out=rs[:], in_=rc[:])
+                else:
+                    nc.sync.dma_start(out=out_0[b, ct * P:(ct + 1) * P, :], in_=acc[:, 0:N])
+                    am = small.tile([P, 1], F32, name="am", tag="am")
+                    nc.vector.tensor_reduce(out=am[:], in_=acc[:, 0:N], axis=AX.X, op=ALU.max, apply_absolute_value=True)
+                    nc.vector.reciprocal(out=rc[:], in_=am[:])
+                    nc.scalar.activation(out=rs[:], in_=rc[:], func=ACT.Copy, scale=448.0)
                 o8 = back.tile([P, N], FP8, name="o8", tag="o8", bufs=4)
                 cut = (N, N // 2, 0)[split]
                 if cut > 0:
@@ -489,6 +498,8 @@ def tile_causalwaveletfieldattentionbyte_pa_kernel(tc, x, k_w, k_b, v_w, v_b, sc
             for b in range(B):
                 hacc = back.tile([P, N], F32, name="hacc%d" % b, tag="hacc%d" % b, bufs=1)
                 held_accs.append(hacc)
+                ham = back.tile([P, 2], F32, name="ham%d" % b, tag="ham%d" % b, bufs=1)
+                held_am.append(ham)
             for k in range(4):
                 k1, k0 = divmod(k, 2)
                 nat_turn_f(HELD, k0, k1, held_fts[k0], "tp")

@@ -188,6 +188,8 @@ def tile_causalwaveletfieldattentionbyte_pa_kernel(tc, x, k_w, k_b, v_w, v_b, sc
             nc.scalar.activation(out=m_sb[:, tau, qu * 4:(qu + 1) * 4], in_=msq[:], func=ACT.Sqrt)
             for h4 in range(4):
                 h = qu * 4 + h4
+                if qu == 0 and h // 2 in NAT:
+                    continue
                 if h // 2 in NAT:
                     dst = f_nat[h // 2][:, tau, (h % 2) * HD:(h % 2 + 1) * HD]
                 else:
@@ -197,6 +199,13 @@ def tile_causalwaveletfieldattentionbyte_pa_kernel(tc, x, k_w, k_b, v_w, v_b, sc
                     in_=kvt[:, 1, h4 * HD:(h4 + 1) * HD],
                     func=ACT.Copy,
                     scale=m_sb[:, tau, h:h + 1],
+                )
+            if qu == 0:
+                nc.gpsimd.tensor_tensor(
+                    out=f_nat[HELD][:, tau, :].rearrange("p (a c) -> p a c", a=2),
+                    in0=kvt[:, 1, P:2 * P].rearrange("p (a c) -> p a c", a=2),
+                    in1=m_sb[:, tau, 2 * HELD:2 * HELD + 2].unsqueeze(2).to_broadcast([P, 2, HD]),
+                    op=ALU.mult,
                 )
 
         def front_units(tg, qu):

@@ -188,7 +188,7 @@ def tile_causalwaveletfieldattentionbyte_pa_kernel(tc, x, k_w, k_b, v_w, v_b, sc
             nc.scalar.activation(out=m_sb[:, tau, qu * 4:(qu + 1) * 4], in_=msq[:], func=ACT.Sqrt)
             for h4 in range(4):
                 h = qu * 4 + h4
-                if qu == 0 and h // 2 in NAT:
+                if qu == 0:
                     continue
                 if h // 2 in NAT:
                     dst = f_nat[h // 2][:, tau, (h % 2) * HD:(h % 2 + 1) * HD]
@@ -201,6 +201,13 @@ def tile_causalwaveletfieldattentionbyte_pa_kernel(tc, x, k_w, k_b, v_w, v_b, sc
                     scale=m_sb[:, tau, h:h + 1],
                 )
             if qu == 0:
+                slots = f_sb[:, tau % 8, 0:2].rearrange("p i s c -> p (i s) c")
+                nc.vector.tensor_tensor(
+                    out=slots[:, 0:4:3, :] if tau // 8 == 0 else slots[:, 1:3, :],
+                    in0=kvt[:, 1, 0:P].rearrange("p (a c) -> p a c", a=2),
+                    in1=m_sb[:, tau, 0:2].unsqueeze(2).to_broadcast([P, 2, HD]),
+                    op=ALU.mult,
+                )
                 nc.gpsimd.tensor_tensor(
                     out=f_nat[HELD][:, tau, :].rearrange("p (a c) -> p a c", a=2),
                     in0=kvt[:, 1, P:2 * P].rearrange("p (a c) -> p a c", a=2),

@@ -26,6 +26,7 @@ YTB = 4
 HELD = 1
 NAT = (1, 7)
 FH = tuple(h for h in range(H) if h // 2 not in NAT)
+PE_ADDS = ((1, 0), (0, 1), (1, 1))
 NATB = 3
 NPASS = D // 512
 NCT = C // P
@@ -403,11 +404,26 @@ def tile_causalwaveletfieldattentionbyte_pa_kernel(tc, x, k_w, k_b, v_w, v_b, sc
 
             def nat_turn_y(ct, b, hi, yts, ft, acc):
                 yp = psum.tile([P, 4, P], F32, name="yp", tag="yt", bufs=YTB)
-                for r in range(4):
-                    nc.tensor.transpose(yp[:, r, :], yts[:, b, hi * 4 + r, :], ident[:])
                 part = acc[:, hi * 512:(hi + 1) * 512].rearrange("p (q r) -> p q r", r=4)
+                in_psum = ct == HELD and (b, hi) in PE_ADDS
+                if in_psum:
+                    nc.tensor.matmul(
+                        out=yp[:].rearrange("p r q -> p q r"),
+                        lhsT=ident[:],
+                        rhs=part,
+                        start=True,
+                        stop=False,
+                    )
+                for r in range(4):
+                    if in_psum:
+                        nc.tensor.matmul(out=yp[:, r, :], lhsT=yts[:, b, hi * 4 + r, :], rhs=ident[:], is_transpose=True, start=False, stop=(r == 3))
+                    else:
+                        nc.tensor.transpose(yp[:, r, :], yts[:, b, hi * 4 + r, :], ident[:])
                 if ct == HELD:
-                    nc.vector.tensor_tensor(out=part, in0=part, in1=yp[:].rearrange("p r q -> p q r"), op=ALU.add)
+                    if in_psum:
+                        nc.scalar.copy(out=part, in_=yp[:].rearrange("p r q -> p q r"))
+                    else:
+                        nc.vector.tensor_tensor(out=part, in0=part, in1=yp[:].rearrange("p r q -> p q r"), op=ALU.add)
                     half = slice(hi * 512, (hi + 1) * 512)
                     nc.sync.dma_start(out=out_0[b, ct * P:(ct + 1) * P, half], in_=acc[:, half])
                     nc.vector.tensor_reduce(out=held_am[b][:, hi:hi + 1], in_=acc[:, half], axis=AX.X, op=ALU.max, apply_absolute_value=True)
@@ -445,7 +461,7 @@ def tile_causalwaveletfieldattentionbyte_pa_kernel(tc, x, k_w, k_b, v_w, v_b, sc
                 ct = t[0]
                 if ct == HELD:
                     if part == 0:
-                        nat_close(ct, i2, t[3][i2], 1 + i2)
+                        nat_close(ct, i2, t[3][i2], 2)
                     return
                 tabs = (cp, cq) if ct in NAT else (cph, cqh)
                 col = ct if ct in NAT else 2 * ct + i2

@@ -27,6 +27,7 @@ HELD = 1
 NAT = (1, 7)
 FH = tuple(h for h in range(H) if h // 2 not in NAT)
 PE_ADDS = ((1, 0), (0, 1), (1, 1))
+KVTB = 4
 NATB = 3
 NPASS = D // 512
 NCT = C // P
@@ -179,7 +180,7 @@ def tile_causalwaveletfieldattentionbyte_pa_kernel(tc, x, k_w, k_b, v_w, v_b, sc
             kv = psum.tile([P, 2, QW], F32, name="kv", tag="mx", bufs=MXB)
             mx_group(kv[:, 0, :], tau, kw_codes, kw_sc, qu * QW)
             mx_group(kv[:, 1, :], tau, vw_codes, vw_sc, qu * QW)
-            kvt = work.tile([P, 2, QW], F32, name="kvt", tag="kvt")
+            kvt = work.tile([P, 2, QW], F32, name="kvt", tag="kvt", bufs=KVTB)
             nc.vector.tensor_tensor(out=kvt[:], in0=kv[:], in1=kvb[:, :, qu * QW:(qu + 1) * QW], op=ALU.add)
             ksq = work.tile([P, QW], F32, name="ksq", tag="ksq")
             msq = work.tile([P, 4], F32, name="msq", tag="msq")

from contextlib import ExitStack

import concourse.mybir as mybir
from concourse.masks import make_identity

B, N, D, C, H, NS = 2, 1024, 1024, 1024, 16, 10
HD = C // H
T0, T1, T2, T3 = 0.4829629131445341, 0.8365163037378079, 0.2241438680420134, -0.1294095225512604

FLOPS = 2 * (B * N) * D * (2 * C) + 2 * B * C * N * 4 * NS

F32 = mybir.dt.float32
BF16 = mybir.dt.bfloat16
U32 = mybir.dt.uint32
U8 = mybir.dt.uint8
FP8X4 = mybir.dt.float8_e4m3fn_x4
FP8 = mybir.dt.float8_e4m3fn
ALU = mybir.AluOpType
ACT = mybir.ActivationFunctionType
AX = mybir.AxisListType

P = 128
MXB = 3
TPB = 1
YTB = 4
HELD = 1
NAT = (1, 7)
FH = tuple(h for h in range(H) if h // 2 not in NAT)
PE_ADDS = ((1, 0), (0, 1), (1, 1))
KVTB = 4
NATB = 3
NPASS = D // 512
NCT = C // P
NTG = B * 2


def tile_causalwaveletfieldattentionbyte_pa_kernel(tc, x, k_w, k_b, v_w, v_b, scale_gain, out_0, out_1):
    nc = tc.nc
    with ExitStack() as ctx:
        const = ctx.enter_context(tc.tile_pool(name="const", bufs=1))
        keep = ctx.enter_context(tc.tile_pool(name="keep", bufs=1))
        work = ctx.enter_context(tc.tile_pool(name="work", bufs=3))
        psum = ctx.enter_context(tc.psum_pool(name="psum", bufs=1))

        ident = const.tile([P, P], F32, name="ident", tag="ident")
        make_identity(nc, ident[:])
        e2 = const.tile([P, 2], F32, name="e2", tag="e2")
        nc.vector.memset(e2[:], 0.0)
        nc.vector.memset(e2[0:64, 0:1], 1.0)
        nc.vector.memset(e2[64:128, 1:2], 1.0)
        zero = const.tile([P, 1], F32, name="zero", tag="zero")
        nc.vector.memset(zero[:], 0.0)

        ipq = const.tile([P, 288], F32, name="ipq", tag="ipq")
        nc.gpsimd.memset(ipq[:], 0.0)
        nc.vector.tensor_reduce(out=ipq[:, 128:160], in_=ident[:].rearrange("p (a s) -> p s a", a=4), axis=AX.X, op=ALU.add)
        e4 = const.tile([P, 4], F32, name="e4", tag="e4")
        nc.vector.tensor_reduce(out=e4[:], in_=ident[:].rearrange("p (a s) -> p a s", a=4), axis=AX.X, op=ALU.add)

        sg_bf = const.tile([P, NS * H], BF16, name="sg_bf", tag="sg_bf")
        nc.sync.dma_start(out=sg_bf[:], in_=scale_gain.rearrange("j h -> (j h)").partition_broadcast(P))
        kvb = const.tile([P, 2, C], BF16, name="kvb", tag="kvb")

        sg = const.tile([P, NS, H], F32, name="sg", tag="sg")
        mx = const.tile([P, H], F32, name="mx", tag="mx")
        ex = const.tile([P, NS, H], F32, name="ex", tag="ex")
        sm = const.tile([P, H], F32, name="sm", tag="sm")
        rsm = const.tile([P, H], F32, name="rsm", tag="rsm")
        gall = const.tile([P, NS, H], F32, name="gall", tag="gall")
        gs = const.tile([P, NS, NCT], F32, name="gs", tag="gs")
        cp = const.tile([P, NS, NCT], F32, name="cp", tag="cp")
        cq = const.tile([P, NS, NCT], F32, name="cq", tag="cq")
        gq = const.tile([P, NS, 4], F32, name="gq", tag="gq")
        cph = const.tile([P, NS, H], F32, name="cph", tag="cph")
        cqh = const.tile([P, NS, H], F32, name="cqh", tag="cqh")

        def gains():
            nc.vector.tensor_copy(out=sg[:].rearrange("p j h -> p (j h)"), in_=sg_bf[:])
            nc.vector.tensor_reduce(out=mx[:], in_=sg[:].rearrange("p j h -> p h j"), axis=AX.X, op=ALU.max)
            nc.vector.tensor_tensor(out=sg[:], in0=sg[:], in1=mx[:].unsqueeze(1).to_broadcast([P, NS, H]), op=ALU.subtract)
            nc.scalar.activation(out=ex[:], in_=sg[:], func=ACT.Exp)
            nc.vector.tensor_reduce(out=sm[:], in_=ex[:].rearrange("p j h -> p h j"), axis=AX.X, op=ALU.add)
            nc.vector.reciprocal(out=rsm[:], in_=sm[:])
            nc.vector.tensor_tensor(out=gall[:], in0=ex[:], in1=rsm[:].unsqueeze(1).to_broadcast([P, NS, H]), op=ALU.mult)
            gv = gall[:].rearrange("p j (ct two) -> p j ct two", two=2)
            nc.vector.tensor_scalar(out=gs[:], in0=gv[:, :, :, 0], scalar1=e2[:, 0:1], scalar2=None, op0=ALU.mult)
            nc.vector.scalar_tensor_tensor(out=gs[:], in0=gv[:, :, :, 1], scalar=e2[:, 1:2], in1=gs[:], op0=ALU.mult, op1=ALU.add)
            nc.vector.tensor_scalar(out=cp[:], in0=gs[:], scalar1=T2, scalar2=None, op0=ALU.mult)
            nc.vector.scalar_tensor_tensor(out=cp[:, 1:NS, :], in0=gs[:, 0:NS - 1, :], scalar=T1, in1=cp[:, 1:NS, :], op0=ALU.mult, op1=ALU.add)
            nc.vector.tensor_scalar(out=cq[:], in0=gs[:], scalar1=T0, scalar2=None, op0=ALU.mult)
            nc.vector.tensor_scalar(out=cph[:], in0=gall[:], scalar1=T2, scalar2=None, op0=ALU.mult)
            nc.vector.scalar_tensor_tensor(out=cph[:, 1:NS, :], in0=gall[:, 0:NS - 1, :], scalar=T1, in1=cph[:, 1:NS, :], op0=ALU.mult, op1=ALU.add)
            nc.vector.tensor_scalar(out=cqh[:], in0=gall[:], scalar1=T0, scalar2=None, op0=ALU.mult)
            gv4 = gall[:].rearrange("p j (q a) -> p j q a", a=4)
            nc.vector.tensor_scalar(out=gq[:], in0=gv4[:, :, :, 0], scalar1=e4[:, 0:1], scalar2=None, op0=ALU.mult)
            for a in range(1, 4):
                nc.vector.scalar_tensor_tensor(out=gq[:], in0=gv4[:, :, :, a], scalar=e4[:, a:a + 1], in1=gq[:], op0=ALU.mult, op1=ALU.add)

        x_codes = keep.tile([P, NPASS, B * N], U32, name="x_codes", tag="x_codes", align_bytes=64)
        x_sc = keep.tile([P, NPASS, B * N], U8, name="x_sc", tag="x_sc", align_bytes=64)
        kw_codes = keep.tile([P, NPASS, C], U32, name="kw_codes", tag="kw_codes", align_bytes=64)
        kw_sc = keep.tile([P, NPASS, C], U8, name="kw_sc", tag="kw_sc", align_bytes=64)
        vw_codes = keep.tile([P, NPASS, C], U32, name="vw_codes", tag="vw_codes", align_bytes=64)
        vw_sc = keep.tile([P, NPASS, C], U8, name="vw_sc", tag="vw_sc", align_bytes=64)
        m_sb = keep.tile([P, NTG * 4, H], F32, name="m_sb", tag="m_sb")
        f_sb = keep.tile([P, 8, len(FH), B, HD], F32, name="f_sb", tag="f_sb")
        f_nat = {}
        for ct in NAT:
            fn = keep.tile([P, NTG * 4, P], F32, name="f_nat%d" % ct, tag="f_nat%d" % ct)
            f_nat[ct] = fn
        taps_of = {1: ((1, T1),)}
        for j in range(2, NS):
            dq = 2 ** (j - 2)
            taps_of[j] = tuple((m * dq, t) for (m, t) in ((1, T2), (2, T1), (3, T0)) if m * dq < 256)
        grange = {}
        gmat = {}
        for j in range(1, NS):
            lo = 96 + taps_of[j][0][0]
            hi = 128 + taps_of[j][-1][0]
            grange[j] = (lo, hi)
            gj = keep.tile([P, hi - lo], F32, name="g%d" % j, tag="g%d" % j)
            gmat[j] = gj
        strip = []
        ttq = []
        for hq in range(4):
            st = keep.tile([P, 352], F32, name="strip%d" % hq, tag="strip%d" % hq)
            nc.gpsimd.memset(st[:], 0.0)
            strip.append(st)
            tq = keep.tile([P, 4, 256], F32, name="ttq%d" % hq, tag="ttq%d" % hq)
            ttq.append(tq)

        def diag(d, lo, hi):
            return ipq[:, lo - d + 32:hi - d + 32]

        def build_masks():
            for j in range(1, NS):
                lo, hi = grange[j]
                for i, (d, t) in enumerate(taps_of[j]):
                    if i == 0:
                        nc.vector.tensor_scalar(out=gmat[j][:], in0=diag(d, lo, hi), scalar1=t, scalar2=None, op0=ALU.mult)
                    else:
                        nc.vector.scalar_tensor_tensor(out=gmat[j][:], in0=diag(d, lo, hi), scalar=t, in1=gmat[j][:], op0=ALU.mult, op1=ALU.add)

        def build_strips():
            for hq in range(4):
                nc.vector.tensor_scalar(out=strip[hq][:, 96:128], in0=diag(0, 96, 128), scalar1=T3, scalar2=None, op0=ALU.mult)
            for j in range(1, NS):
                lo, hi = grange[j]
                for hq in range(4):
                    nc.vector.scalar_tensor_tensor(
                        out=strip[hq][:, lo:hi],
                        in0=gmat[j][:],
                        scalar=gq[:, j, hq:hq + 1],
                        in1=strip[hq][:, lo:hi],
                        op0=ALU.mult,
                        op1=ALU.add,
                    )

        def spread_strips():
            for hq in range(4):
                for a in range(4):
                    for b in range(4):
                        nc.sync.dma_start(out=ttq[hq][32 * b:32 * b + 32, a, :], in_=strip[hq][32 * a:32 * a + 32, 96 - 32 * b:352 - 32 * b])

        QW = C // 4

        def mx_group(ps, tau, r_codes, r_sc, rcol):
            for g in range(NPASS):
                nc.tensor.matmul_mx(
                    out=ps,
                    lhsT=x_codes[:, g, tau * P:(tau + 1) * P].bitcast(FP8X4),
                    lhsT_scale=x_sc[:, g, tau * P:(tau + 1) * P],
                    rhs=r_codes[:, g, rcol:rcol + QW].bitcast(FP8X4),
                    rhs_scale=r_sc[:, g, rcol:rcol + QW],
                    start=(g == 0),
                    stop=(g == NPASS - 1),
                )

        def kv_unit(tau, qu):
            kv = psum.tile([P, 2, QW], F32, name="kv", tag="mx", bufs=MXB)
            mx_group(kv[:, 0, :], tau, kw_codes, kw_sc, qu * QW)
            mx_group(kv[:, 1, :], tau, vw_codes, vw_sc, qu * QW)
            kvt = work.tile([P, 2, QW], F32, name="kvt", tag="kvt", bufs=KVTB)
            nc.vector.tensor_tensor(out=kvt[:], in0=kv[:], in1=kvb[:, :, qu * QW:(qu + 1) * QW], op=ALU.add)
            ksq = work.tile([P, QW], F32, name="ksq", tag="ksq")
            msq = work.tile([P, 4], F32, name="msq", tag="msq")
            for h4 in range(4):
                hs = slice(h4 * HD, (h4 + 1) * HD)
                nc.scalar.activation(out=ksq[:, hs], in_=kvt[:, 0, hs], func=ACT.Square, accum_out=msq[:, h4:h4 + 1])
            nc.scalar.activation(out=m_sb[:, tau, qu * 4:(qu + 1) * 4], in_=msq[:], func=ACT.Sqrt)
            for h4 in range(4):
                h = qu * 4 + h4
                if qu == 0:
                    continue
                if h // 2 in NAT:
                    dst = f_nat[h // 2][:, tau, (h % 2) * HD:(h % 2 + 1) * HD]
                else:
                    dst = f_sb[:, tau % 8, FH.index(h), (tau // 8 + h) % 2, :]
                nc.scalar.activation(
                    out=dst,
                    in_=kvt[:, 1, h4 * HD:(h4 + 1) * HD],
                    func=ACT.Copy,
                    scale=m_sb[:, tau, h:h + 1],
                )
            if qu == 0:
                slots = f_sb[:, tau % 8, 0:2].rearrange("p i s c -> p (i s) c")
                nc.vector.tensor_tensor(
                    out=slots[:, 0:4:3, :] if tau // 8 == 0 else slots[:, 1:3, :],
                    in0=kvt[:, 1, 0:P].rearrange("p (a c) -> p a c", a=2),
                    in1=m_sb[:, tau, 0:2].unsqueeze(2).to_broadcast([P, 2, HD]),
                    op=ALU.mult,
                )
                nc.gpsimd.tensor_tensor(
                    out=f_nat[HELD][:, tau, :].rearrange("p (a c) -> p a c", a=2),
                    in0=kvt[:, 1, P:2 * P].rearrange("p (a c) -> p a c", a=2),
                    in1=m_sb[:, tau, 2 * HELD:2 * HELD + 2].unsqueeze(2).to_broadcast([P, 2, HD]),
                    op=ALU.mult,
                )

        def front_units(tg, qu):
            pieces = []
            for r in range(4):
                pieces.append((lambda tau: kv_unit(tau, qu), tg * 4 + r))
            return pieces

        def run(pieces):
            for (fn, arg) in pieces:
                fn(arg)

        def w_view(w, half):
            return w[512 * half:512 * (half + 1), :].rearrange("(s j) d -> j s d", j=P)

        def prep_pass(raw, codes, scales, col0, g, new_grouped):
            grouped = new_grouped()
            gw = grouped[:].bitcast(F32).rearrange("p (s j u) -> p s j u", s=4, u=2)
            for a in range(2):
                xt = psum.tile([P, 2, 2, P], F32, name="xt", tag="yt", bufs=YTB)
                for s2 in range(2):
                    words = raw[:, 2 * a + s2, :].bitcast(F32)
                    for u in range(2):
                        nc.tensor.transpose(xt[:, s2, u, :], words[:, 256 * g + u:256 * (g + 1):2], ident[:])
                nc.scalar.copy(out=gw[:, 2 * a:2 * a + 2], in_=xt[:].rearrange("p s u j -> p s j u"))
            nc.vector.quantize_mx(
                out=codes[:, g, col0:col0 + 512].bitcast(FP8X4),
                scales=scales[:, g, col0:col0 + 512],
                in_=grouped[:],
            )

        raw_late = []
        with ExitStack() as front:
            raw_pool = front.enter_context(tc.tile_pool(name="raw", bufs=6))
            grp = front.enter_context(tc.tile_pool(name="grp", bufs=3))

            def load(view, nm):
                t = raw_pool.tile([P, 4, D], BF16, name=nm, tag="raw")
                for a in range(2):
                    nc.sync.dma_start(out=t[:, 2 * a:2 * a + 2, :], in_=view[:, 2 * a:2 * a + 2, :])
                return t

            def x_view(tg):
                b, hi = divmod(tg, 2)
                return x[b, 512 * hi:512 * (hi + 1), :].rearrange("(q r) d -> q r d", r=4)

            raw_kw0 = load(w_view(k_w, 0), "raw_kw0")
            raw_x = [load(x_view(0), "raw_x0")]
            nc.sync.dma_start(out=kvb[:, 0, :], in_=k_b.partition_broadcast(P))
            raw_vw0 = load(w_view(v_w, 0), "raw_vw0")
            nc.sync.dma_start(out=kvb[:, 1, :], in_=v_b.partition_broadcast(P))
            for tg in range(1, NTG):
                raw_x.append(load(x_view(tg), "raw_x%d" % tg))
            for (w, nm) in ((k_w, "raw_kw1"), (v_w, "raw_vw1")):
                rl = keep.tile([P, 4, D], BF16, name=nm, tag="yts", bufs=2)
                for a in range(2):
                    nc.sync.dma_start(out=rl[:, 2 * a:2 * a + 2, :], in_=w_view(w, 1)[:, 2 * a:2 * a + 2, :])
                raw_late.append(rl)

            def front_grouped():
                grouped = grp.tile([P, 2048], BF16, name="grouped", tag="grouped", align_bytes=64)
                return grouped

            def prep(raw, codes, scales, col0):
                for g in range(NPASS):
                    prep_pass(raw, codes, scales, col0, g, front_grouped)

            build_masks()
            prep(raw_kw0, kw_codes, kw_sc, 0)
            prep(raw_x[0], x_codes, x_sc, 0)
            prep(raw_vw0, vw_codes, vw_sc, 0)
            gains()
            build_strips()
            spread_strips()
            prep(raw_x[1], x_codes, x_sc, 512)
            run(front_units(0, 0))
            prep(raw_x[2], x_codes, x_sc, 1024)
            run(front_units(1, 0))
            prep(raw_x[3], x_codes, x_sc, 1536)
            run(front_units(2, 0))
            run(front_units(3, 0))

        PAD = 8
        vtaps = ((2, 0, 1), (3, 1, 0), (6, 1, 1))

        with ExitStack() as rear:
            back = rear.enter_context(tc.tile_pool(name="back", bufs=3))
            small = rear.enter_context(tc.tile_pool(name="small", bufs=4))
            ft_bufs = []
            for i in range(6):
                ftb = back.tile([P, PAD + N], F32, name="ft%d" % i, tag="ft%d" % i, bufs=1)
                nc.gpsimd.memset(ftb[:, 0:PAD], 0.0)
                ft_bufs.append(ftb)

            def late_grouped():
                grouped = back.tile([P, 2048], BF16, name="grouped2", tag="nat", bufs=NATB, align_bytes=64)
                return grouped

            def late_prep(i):
                prep_pass(raw_late[i // 2], (kw_codes, vw_codes)[i // 2], (kw_sc, vw_sc)[i // 2], 512, i % 2, late_grouped)

            def f_tile(h, hi, r):
                return f_sb[:, hi * 4 + r, FH.index(h)].rearrange("p s c -> p (s c)")

            def turn_f(h, hi, ft, tag):
                tp = psum.tile([P, 4, P], F32, name="tp", tag=tag, bufs=(TPB if tag == "tp" else MXB))
                for r in range(4):
                    nc.tensor.transpose(tp[:, r, :], f_tile(h, hi, r), ident[:])
                nc.scalar.copy(
                    out=ft[:, PAD + hi * 512:PAD + (hi + 1) * 512].rearrange("p (q r) -> p q r", r=4),
                    in_=tp[:].rearrange("p r q -> p q r"),
                )

            def toep(h, hi, y, phases):
                th = ttq[h // 4][:, h % 4, :]
                for r in phases:
                    if hi == 0:
                        nc.tensor.matmul(out=y[:, r, :], lhsT=f_tile(h, 0, r), rhs=th[:, 0:P], start=True, stop=True)
                    else:
                        nc.tensor.matmul(out=y[:, r, :], lhsT=f_tile(h, 0, r), rhs=th[:, P:2 * P], start=True, stop=False)
                        nc.tensor.matmul(out=y[:, r, :], lhsT=f_tile(h, 1, r), rhs=th[:, 0:P], start=False, stop=True)

            def first_tap(h, hi, y, ft, acc):
                nc.vector.scalar_tensor_tensor(
                    out=acc[:, hi * 512:(hi + 1) * 512].rearrange("p (q r) -> p q r", r=4),
                    in0=ft[:, PAD - 1 + hi * 512:PAD - 1 + (hi + 1) * 512].rearrange("p (q r) -> p q r", r=4),
                    scalar=cph[:, 0, h:h + 1],
                    in1=y[:].rearrange("p r q -> p q r"),
                    op0=ALU.mult,
                    op1=ALU.add,
                )

            def tap1(tabs, col, ft, acc, i):
                (o, w, j) = vtaps[i]
                nc.vector.scalar_tensor_tensor(out=acc[:, 0:N], in0=ft[:, PAD - o:PAD - o + N], scalar=tabs[w][:, j, col:col + 1], in1=acc[:, 0:N], op0=ALU.mult, op1=ALU.add)

            def close_head(t, h2):
                ct = t[0]
                h = 2 * ct + h2
                acc = t[3][h2]
                nc.sync.dma_start(out=out_0[0, h * HD:(h + 1) * HD, :], in_=acc[h2 * HD:(h2 + 1) * HD, 0:N])
                am = small.tile([P, 1], F32, name="am", tag="am")
                nc.vector.tensor_reduce(out=am[:], in_=acc[:, 0:N], axis=AX.X, op=ALU.max, apply_absolute_value=True)
                rc = small.tile([P, 1], F32, name="rc", tag="rc")
                nc.vector.reciprocal(out=rc[:], in_=am[:])
                nc.scalar.activation(out=acc[:, N:N + 1], in_=rc[:], func=ACT.Copy, scale=448.0)
                if h2 == 0:
                    o8a = back.tile([P, N], FP8, name="o8a", tag="o8", bufs=4)
                    nat = back.tile([P, N + 1], F32, name="nat", tag="nat", bufs=NATB, align_bytes=64)
                    t[4]["o8a"] = o8a
                    t[4]["nat"] = nat
                o8a = t[4]["o8a"]
                nat = t[4]["nat"]
                lane = slice(h2 * HD, (h2 + 1) * HD)
                other = slice((1 - h2) * HD, (2 - h2) * HD)
                nc.sync.dma_start(out=nat[lane, :], in_=acc[other, :])
                nc.scalar.activation(out=o8a[lane, :], in_=acc[lane, 0:N], func=ACT.Identity, bias=zero[lane, 0:1], scale=acc[lane, N:N + 1], saturate=False)
                if h2 == 1:
                    nc.sync.dma_start(out=out_1[0, ct * P:(ct + 1) * P, :], in_=o8a[:].bitcast(U8))
                    nc.sync.dma_start(out=out_0[1, ct * P:(ct + 1) * P, :], in_=nat[:, 0:N])
                    o8b = back.tile([P, N], FP8, name="o8b", tag="o8", bufs=4)
                    nc.scalar.activation(out=o8b[:], in_=nat[:, 0:N], func=ACT.Identity, bias=zero[:, 0:1], scale=nat[:, N:N + 1], saturate=False)
                    nc.sync.dma_start(out=out_1[1, ct * P:(ct + 1) * P, :], in_=o8b[:].bitcast(U8))

            def nat_toeplitz(ct, h2, hi, yts):
                h = 2 * ct + h2
                cols = slice(h2 * HD, (h2 + 1) * HD)
                th = ttq[h // 4][:, h % 4, :]
                fn5 = f_nat[ct][:].rearrange("p (b a r) c -> p b a r c", b=B, a=2)
                yt = psum.tile([P, B, 4, HD], F32, name="yt", tag="yt", bufs=YTB)
                if hi == 0:
                    nc.tensor.matmul(out=yt[:], lhsT=th[:, 0:P], rhs=fn5[:, :, 0, :, cols], start=True, stop=True)
                else:
                    nc.tensor.matmul(out=yt[:], lhsT=th[:, 0:P], rhs=fn5[:, :, 1, :, cols], start=True, stop=False)
                    nc.tensor.matmul(out=yt[:], lhsT=th[:, P:2 * P], rhs=fn5[:, :, 0, :, cols], start=False, stop=True)
                nc.scalar.copy(out=yts[:, :, hi * 4:(hi + 1) * 4, cols], in_=yt[:])

            def nat_turn_f(ct, b, hi, ft, tag):
                tp = psum.tile([P, 4, P], F32, name="tp", tag=tag, bufs=(TPB if tag == "tp" else MXB))
                for r in range(4):
                    nc.tensor.transpose(tp[:, r, :], f_nat[ct][:, (b * 2 + hi) * 4 + r, :], ident[:])
                nc.scalar.copy(
                    out=ft[:, PAD + hi * 512:PAD + (hi + 1) * 512].rearrange("p (q r) -> p q r", r=4),
                    in_=tp[:].rearrange("p r q -> p q r"),
                )

            held_am = []

            def nat_turn_y(ct, b, hi, yts, ft, acc):
                yp = psum.tile([P, 4, P], F32, name="yp", tag="yt", bufs=YTB)
                part = acc[:, hi * 512:(hi + 1) * 512].rearrange("p (q r) -> p q r", r=4)
                in_psum = ct == HELD and (b, hi) in PE_ADDS
                if in_psum:
                    nc.tensor.matmul(
                        out=yp[:].rearrange("p r q -> p q r"),
                        lhsT=ident[:],
                        rhs=part,
                        start=True,
                        stop=False,
                    )
                for r in range(4):
                    if in_psum:
                        nc.tensor.matmul(out=yp[:, r, :], lhsT=yts[:, b, hi * 4 + r, :], rhs=ident[:], is_transpose=True, start=False, stop=(r == 3))
                    else:
                        nc.tensor.transpose(yp[:, r, :], yts[:, b, hi * 4 + r, :], ident[:])
                if ct == HELD:
                    if in_psum:
                        nc.scalar.copy(out=part, in_=yp[:].rearrange("p r q -> p q r"))
                    else:
                        nc.vector.tensor_tensor(out=part, in0=part, in1=yp[:].rearrange("p r q -> p q r"), op=ALU.add)
                    half = slice(hi * 512, (hi + 1) * 512)
                    nc.sync.dma_start(out=out_0[b, ct * P:(ct + 1) * P, half], in_=acc[:, half])
                    nc.vector.tensor_reduce(out=held_am[b][:, hi:hi + 1], in_=acc[:, half], axis=AX.X, op=ALU.max, apply_absolute_value=True)
                    return
                nc.vector.scalar_tensor_tensor(
                    out=part,
                    in0=ft[:, PAD - 1 + hi * 512:PAD - 1 + (hi + 1) * 512].rearrange("p (q r) -> p q r", r=4),
                    scalar=cp[:, 0, ct:ct + 1],
                    in1=yp[:].rearrange("p r q -> p q r"),
                    op0=ALU.mult,
                    op1=ALU.add,
                )

            def nat_close(ct, b, acc, split):
                rc = small.tile([P, 1], F32, name="rc", tag="rc")
                rs = small.tile([P, 1], F32, name="rs", tag="rs")
                if ct == HELD:
                    nc.vector.tensor_scalar(out=rc[:], in0=held_am[b][:, 0:1], scalar1=held_am[b][:, 1:2], scalar2=1.0 / 448.0, op0=ALU.max, op1=ALU.mult)
                    nc.vector.reciprocal(out=rs[:], in_=rc[:])
                else:
                    nc.sync.dma_start(out=out_0[b, ct * P:(ct + 1) * P, :], in_=acc[:, 0:N])
                    am = small.tile([P, 1], F32, name="am", tag="am")
                    nc.vector.tensor_reduce(out=am[:], in_=acc[:, 0:N], axis=AX.X, op=ALU.max, apply_absolute_value=True)
                    nc.vector.reciprocal(out=rc[:], in_=am[:])
                    nc.scalar.activation(out=rs[:], in_=rc[:], func=ACT.Copy, scale=448.0)
                o8 = back.tile([P, N], FP8, name="o8", tag="o8", bufs=4)
                cut = (N, N // 2, 0)[split]
                if cut > 0:
                    nc.scalar.activation(out=o8[:, 0:cut], in_=acc[:, 0:cut], func=ACT.Identity, bias=zero[:, 0:1], scale=rs[:, 0:1], saturate=False)
                if cut < N:
                    nc.vector.tensor_scalar(out=o8[:, cut:N], in0=acc[:, cut:N], scalar1=rs[:, 0:1], scalar2=None, op0=ALU.mult, saturate=False)
                nc.sync.dma_start(out=out_1[b, ct * P:(ct + 1) * P, :], in_=o8[:].bitcast(U8))

            def fin_tile(t, i2, part):
                ct = t[0]
                if ct == HELD:
                    if part == 0:
                        nat_close(ct, i2, t[3][i2], 2)
                    return
                tabs = (cp, cq) if ct in NAT else (cph, cqh)
                col = ct if ct in NAT else 2 * ct + i2
                if part == 0:
                    tap1(tabs, col, t[2][i2], t[3][i2], 0)
                    tap1(tabs, col, t[2][i2], t[3][i2], 1)
                else:
                    tap1(tabs, col, t[2][i2], t[3][i2], 2)
                    if ct in NAT:
                        nat_close(ct, i2, t[3][i2], 0)
                    else:
                        close_head(t, i2)

            def start_pair(ct, place):
                prod = {}
                if ct in NAT:
                    prod = keep.tile([P, B, 8, P], F32, name="yts", tag="yts", bufs=2)
                if ct == HELD:
                    return (ct, prod, held_fts, held_accs, {})
                accs = []
                for i2 in range(2):
                    acc = back.tile([P, N + 1], F32, name="acc", tag="acc", bufs=5)
                    accs.append(acc)
                return (ct, prod, (ft_bufs[(2 * place) % 6], ft_bufs[(2 * place + 1) % 6]), accs, {})

            def empty(t, i2, hi):
                if t[0] in NAT:
                    nat_turn_y(t[0], i2, hi, t[1], t[2][i2], t[3][i2])
                else:
                    first_tap(2 * t[0] + i2, hi, t[1][(i2, hi)], t[2][i2], t[3][i2])

            def weave(cur, nxt, units, tp_tag):
                for k in range(4):
                    k1, k0 = divmod(k, 2)
                    if k < 2 and cur is not None:
                        empty(cur, k0, 1)
                    if k >= 2 and nxt is not None:
                        empty(nxt, k0, 0)
                    y = None
                    if nxt is not None:
                        if nxt[0] not in NAT:
                            turn_f(2 * nxt[0] + k0, k1, nxt[2][k0], tp_tag)
                            y = psum.tile([P, 4, P], F32, name="y", tag="yt", bufs=YTB)
                            nxt[1][(k0, k1)] = y
                            toep(2 * nxt[0] + k0, k1, y, (0, 1))
                        else:
                            if nxt[0] != HELD:
                                nat_turn_f(nxt[0], k0, k1, nxt[2][k0], tp_tag)
                            nat_toeplitz(nxt[0], k0, k1, nxt[1])
                    per = len(units) // 4
                    run(units[per * k:per * (k + 1)])
                    if y is not None:
                        toep(2 * nxt[0] + k0, k1, y, (2, 3))
                    if cur is not None:
                        if k in (0, 1):
                            fin_tile(cur, 0, k)
                        else:
                            fin_tile(cur, 1, k - 2)

            late = []
            for qu in range(1, 4):
                for tg in range(NTG):
                    late.extend(front_units(tg, qu))
            held_fts = (ft_bufs[0], ft_bufs[1])
            held_accs = []
            for b in range(B):
                hacc = back.tile([P, N], F32, name="hacc%d" % b, tag="hacc%d" % b, bufs=1)
                held_accs.append(hacc)
                ham = back.tile([P, 2], F32, name="ham%d" % b, tag="ham%d" % b, bufs=1)
                held_am.append(ham)
            for k in range(4):
                k1, k0 = divmod(k, 2)
                nat_turn_f(HELD, k0, k1, held_fts[k0], "tp")
            for b in range(B):
                nc.scalar.activation(out=held_accs[b][:], in_=held_fts[b][:, PAD - 1:PAD - 1 + N], func=ACT.Copy, scale=cp[:, 0, HELD:HELD + 1])
            for i in range(3):
                for b in range(B):
                    tap1((cp, cq), HELD, held_fts[b], held_accs[b], i)
            order = [ct for ct in range(NCT) if ct != HELD] + [HELD]
            shares = (16, 8, 8, 8, 8)
            cur = None
            for pos in range(NCT + 1):
                nxt = start_pair(order[pos], pos + 1) if pos < NCT else None
                first = sum(shares[:pos])
                units = late[first:first + shares[pos]] if pos < len(shares) else []
                if pos == 0:
                    woven = []
                    for k in range(4):
                        woven.extend(units[4 * k:4 * k + 4])
                        woven.append((late_prep, k))
                    units = woven
                weave(cur, nxt, units, "tp" if pos < len(shares) else "mx")
                cur = nxt
